import numpy as np
import ml_dtypes


def mxq(x, axis, fmt="e4m3"):
    dtype, down = {"e4m3": (ml_dtypes.float8_e4m3fn, 7), "e5m2": (ml_dtypes.float8_e5m2, 14)}[fmt]
    v = np.moveaxis(np.asarray(x, np.float32).astype(ml_dtypes.bfloat16).astype(np.float64), axis, -1)
    blocks = v.reshape(v.shape[:-1] + (-1, 32))
    amax = np.abs(blocks).max(-1, keepdims=True)
    byte = np.maximum(np.where(amax > 0, np.frexp(amax)[1] - 1 + 127, 0) - down, 1)
    scale = np.exp2(byte - 127.0)
    codes = (blocks / scale).astype(np.float32).astype(dtype).astype(np.float64)
    return np.moveaxis((codes * scale).reshape(v.shape), -1, axis)


WIDE = False


def mx_kscale(k):
    if not WIDE:
        return np.ones(k)
    levels = np.array([10, -10, 5, -5, 0])
    a = np.random.permutation(np.resize(levels, k // 512 * 4)).reshape(k // 512, 4)
    idx = np.arange(k)
    return np.exp2(a[idx // 512, idx % 128 // 32])


BF16 = ml_dtypes.bfloat16


def bf(x):
    return np.asarray(x, np.float32).astype(BF16)


def f64(x):
    return np.asarray(x).astype(np.float64)


B, I, H, O = 2048, 512, 1024, 512
RHO_OVER_T = 1.68e-8 / 35e-6
MIN_TRACE_W, MAX_TRACE_W = 0.09, 5.0
W_MIN, W_MAX = -3.0, 3.0
BOARD = 2800.0 * np.sqrt(H)


def manhattan(a, b):
    return np.sum(np.abs(a[:, None, :] - b[None, :, :]), axis=-1)


def effective_weight(W, L):
    norm = (np.clip(W, W_MIN, W_MAX) - W_MIN) / (W_MAX - W_MIN)
    width = MIN_TRACE_W + norm * (MAX_TRACE_W - MIN_TRACE_W)
    R = RHO_OVER_T * L / width
    return W * (1.0 / (R + 1.0))


def sigmoid(v):
    return 1.0 / (1.0 + np.exp(-v))


def setup_inputs():
    s = mx_kscale(I)
    x = bf(np.random.standard_normal((B, I)) * 0.23 * np.sqrt(H / I) * s)
    W1 = bf(np.random.standard_normal((I, H)) * 1.5 / s[:, None])
    b1 = bf(np.random.standard_normal(H) * 0.5)
    W2 = bf(np.random.standard_normal((H, O)) * 1.5 - 1.0)
    input_positions = bf(np.random.random((I, 2)) * np.array([0.4 * BOARD, BOARD]))
    hidden_positions = bf(np.random.random((H, 2)) * np.array([0.6 * BOARD, BOARD]) + np.array([0.2 * BOARD, 0.0]))
    output_positions = bf(np.random.random((O, 2)) * np.array([0.4 * BOARD, BOARD]) + np.array([0.6 * BOARD, 0.0]))
    drive = 0.5 * effective_weight(f64(W2), manhattan(f64(hidden_positions), f64(output_positions))).sum(0)
    b2 = bf(np.random.standard_normal(O) * 0.5 - drive)
    return {"x": x, "W1": W1, "b1": b1, "W2": W2, "b2": b2, "input_positions": input_positions,
            "hidden_positions": hidden_positions, "output_positions": output_positions}


def reference(x, W1, b1, W2, b2, input_positions, hidden_positions, output_positions):
    L1 = manhattan(f64(input_positions), f64(hidden_positions))
    L2 = manhattan(f64(hidden_positions), f64(output_positions))
    W1_eff = effective_weight(f64(W1), L1)
    W2_eff = effective_weight(f64(W2), L2)
    hidden = sigmoid((mxq(f64(x), 1, "e4m3") @ mxq(W1_eff, 0, "e4m3")) + f64(b1))
    return sigmoid((mxq(hidden, 1, "e4m3") @ mxq(W2_eff, 0, "e4m3")) + f64(b2))

@@ -1,0 +1,377 @@
+from contextlib import ExitStack
+
+import concourse.mybir as mybir
+from concourse.masks import make_identity
+
+F32 = mybir.dt.float32
+BF16 = mybir.dt.bfloat16
+U32 = mybir.dt.uint32
+U8 = mybir.dt.uint8
+FP8X4 = mybir.dt.float8_e4m3fn_x4
+ACT = mybir.ActivationFunctionType
+ALU = mybir.AluOpType
+
+P = 128
+B, I, H, O = 2048, 512, 1024, 512
+FLOPS = 2 * B * I * H + 2 * B * H * O
+RHO = 1.68e-8 / 35e-6
+WA = (5.0 - 0.09) / 6.0
+WB = 0.09 + (5.0 - 0.09) / 2.0
+EPS = 1e-18
+CH = 256
+ABS2 = (3,)
+
+
+def tile_physicalneuralnetwork_kernel(
+    tc, x, W1, b1, W2, b2, input_positions, hidden_positions, output_positions, out
+):
+    nc = tc.nc
+    with ExitStack() as ctx:
+        const = ctx.enter_context(tc.tile_pool(name="const", bufs=1))
+        w8 = ctx.enter_context(tc.tile_pool(name="w8", bufs=2))
+        a1p = ctx.enter_context(tc.tile_pool(name="a1p", bufs=8))
+        a2p = ctx.enter_context(tc.tile_pool(name="a2p", bufs=3))
+        hp = ctx.enter_context(tc.tile_pool(name="hp", bufs=2))
+        hq = ctx.enter_context(tc.tile_pool(name="hq", bufs=3))
+        op = ctx.enter_context(tc.tile_pool(name="op", bufs=4))
+        psx = ctx.enter_context(tc.psum_pool(name="psx", bufs=2))
+        psa = ctx.enter_context(tc.psum_pool(name="psa", bufs=4))
+        psb = ctx.enter_context(tc.psum_pool(name="psb", bufs=2))
+        ctx.enter_context(nc.allow_non_contiguous_dma(reason="small per-partition vectors"))
+
+        ipos = const.tile([P, 2, 4], BF16)
+        nc.sync.dma_start(
+            out=ipos[:], in_=input_positions.rearrange("(u p e) c -> p u (e c)", u=2, e=2)
+        )
+        hpb = const.tile([P, H, 2], BF16)
+        nc.sync.dma_start(
+            out=hpb[:].rearrange("p h c -> p (h c)"),
+            in_=hidden_positions.rearrange("h c -> (h c)").partition_broadcast(P),
+        )
+        hpos = const.tile([P, 8, 2], BF16)
+        nc.sync.dma_start(out=hpos[:], in_=hidden_positions.rearrange("(a p) c -> p a c", p=P))
+        opb = const.tile([P, O, 2], BF16)
+        nc.sync.dma_start(
+            out=opb[:].rearrange("p h c -> p (h c)"),
+            in_=output_positions.rearrange("h c -> (h c)").partition_broadcast(P),
+        )
+        w1sb = const.tile([P, 4, H], BF16)
+        nc.sync.dma_start(
+            out=w1sb[:].rearrange("p (u e) h -> p u (e h)", u=2),
+            in_=W1.rearrange("(u p e) h -> p u (e h)", u=2, e=2),
+        )
+        xsb = const.tile([P, 16, I], BF16)
+        xv = x.rearrange("(m r) i -> m r i", r=16)
+        nc.sync.dma_start(out=xsb[:, 0:4, :], in_=xv[:, 0:4, :])
+        w2sb = const.tile([P, 8, O], BF16)
+        nc.sync.dma_start(out=w2sb[:], in_=W2.rearrange("(a p) o -> p a o", p=P))
+        for c in range(1, 4):
+            nc.sync.dma_start(out=xsb[:, 4 * c : 4 * c + 4, :], in_=xv[:, 4 * c : 4 * c + 4, :])
+        b1sb = const.tile([P, 8], BF16)
+        nc.sync.dma_start(out=b1sb[:], in_=b1.rearrange("(a p) -> p a", p=P))
+        b2b = const.tile([P, O], BF16)
+        nc.sync.dma_start(out=b2b[:], in_=b2.partition_broadcast(P))
+
+        ident = const.tile([P, P], F32)
+        make_identity(nc, ident[:])
+
+        eps = const.tile([P, 1], F32)
+        nc.vector.memset(eps[:], EPS)
+        one = const.tile([P, 1], F32)
+        nc.vector.memset(one[:], 1.0)
+        warm = const.tile([P, 1], F32)
+        nc.scalar.activation(out=warm[:], in_=one[:], func=ACT.Ln)
+        nip = const.tile([P, 8], F32)
+        nc.vector.tensor_scalar_mul(out=nip[:], in0=ipos[:].rearrange("p u k -> p (u k)"), scalar1=-1.0)
+        hpf = const.tile([P, 8, 2], F32)
+        nc.vector.tensor_copy(out=hpf[:], in_=hpos[:])
+        nhp = const.tile([P, 16], F32)
+        nc.vector.tensor_scalar_mul(out=nhp[:], in0=hpos[:].rearrange("p a c -> p (a c)"), scalar1=-1.0)
+        nhs = const.tile([P, 8], F32)
+        nc.vector.tensor_tensor(out=nhs[:], in0=hpf[:, :, 0], in1=hpf[:, :, 1], op=ALU.add)
+        nc.vector.tensor_scalar_mul(out=nhs[:], in0=nhs[:], scalar1=-0.5)
+        nos = const.tile([P, O], F32)
+        nc.vector.tensor_tensor(out=nos[:], in0=opb[:, :, 0], in1=opb[:, :, 1], op=ALU.add)
+        nc.vector.tensor_scalar_mul(out=nos[:], in0=nos[:], scalar1=-0.5)
+
+        xg = const.tile([P, 16, P, 4], BF16, align_bytes=64)
+        xc = const.tile([P, B], U32, align_bytes=64)
+        xs = const.tile([P, B], U8, align_bytes=64)
+        z1 = const.tile([P, 4, 4, CH], F32)
+        z2 = const.tile([P, 4, 4, CH], F32)
+        c1 = const.tile([P, 4 * CH], U32, align_bytes=64)
+        s1 = const.tile([P, 4 * CH], U8, align_bytes=64)
+        c2 = const.tile([P, 4 * CH], U32, align_bytes=64)
+        s2 = const.tile([P, 4 * CH], U8, align_bytes=64)
+        wc1 = w8.tile([P, 4, H], BF16, name="wc1", tag="w8", align_bytes=64)
+        wc2 = w8.tile([P, 8, O], BF16, name="wc2", tag="w8", align_bytes=64)
+        lt = {}
+
+        def clamp(wc, wsb):
+            nc.vector.tensor_scalar(
+                out=wc[:], in0=wsb[:], scalar1=-3.0, scalar2=3.0, op0=ALU.max, op1=ALU.min
+            )
+
+        def abs_s(key, posb, npos, rows, n):
+            a1 = a1p.tile([P, 1024], F32, name="a1")
+            a2 = a2p.tile([P, 1024], F32, name="a2")
+            lt[key] = (a1, a2)
+            for k, j in enumerate(rows):
+                nc.scalar.activation(
+                    out=a1[:, k * n : (k + 1) * n], in_=posb[:, :, 0], func=ACT.Abs,
+                    bias=npos[:, 2 * j : 2 * j + 1], scale=1.0,
+                )
+                nc.scalar.activation(
+                    out=a2[:, k * n : (k + 1) * n], in_=posb[:, :, 1], func=ACT.Abs,
+                    bias=npos[:, 2 * j + 1 : 2 * j + 2], scale=1.0,
+                )
+
+        def abs_v(key):
+            a1, a2 = lt[key]
+            nc.vector.tensor_tensor(out=a1[:], in0=a1[:], in1=a2[:], op=ALU.add)
+
+        def max_v(key, rows):
+            a1 = a1p.tile([P, 1024], F32, name="a1")
+            lt[key] = (a1, None)
+            for k, j in enumerate(rows):
+                sl = a1[:, k * O : (k + 1) * O]
+                nc.vector.scalar_tensor_tensor(
+                    out=sl, in0=opb[:, :, 0], scalar=hpf[:, j, 0:1], in1=nos[:], op0=ALU.max, op1=ALU.add
+                )
+                nc.vector.scalar_tensor_tensor(
+                    out=sl, in0=opb[:, :, 1], scalar=hpf[:, j, 1:2], in1=sl, op0=ALU.max, op1=ALU.add
+                )
+                nc.vector.tensor_scalar(
+                    out=sl, in0=sl, scalar1=nhs[:, j : j + 1], scalar2=0.0, op0=ALU.add, op1=ALU.max
+                )
+
+        def ln_width(z, wc, g, kper):
+            nc.scalar.activation(
+                out=z[:, g * kper : (g + 1) * kper],
+                in_=wc[:, 4 * g : 4 * g + 4, :].rearrange("p t (k h) -> p k t h", h=CH),
+                func=ACT.Ln, bias=one[:], scale=WA / WB,
+            )
+
+        def ln_len(key, factor):
+            a1 = lt[key][0]
+            nc.scalar.activation(out=a1[:], in_=a1[:], func=ACT.Ln, bias=eps[:], scale=factor * RHO / WB)
+
+        def zed1(q):
+            nc.vector.tensor_tensor(
+                out=z1[:, :, q, :], in0=z1[:, :, q, :],
+                in1=lt[(1, q)][0][:].rearrange("p (k h) -> p k h", h=CH), op=ALU.subtract,
+            )
+
+        def zed2(q):
+            g, t0 = q // 2, 2 * (q % 2)
+            zv = z2[:, 2 * g : 2 * g + 2, t0 : t0 + 2, :]
+            nc.vector.tensor_tensor(
+                out=zv, in0=zv, in1=lt[(2, q)][0][:].rearrange("p (t k h) -> p k t h", t=2, h=CH),
+                op=ALU.subtract,
+            )
+
+        def transposes(pair):
+            xt = psx.tile([P, 2, 2, P], F32, name="xt")
+            for rr in range(2):
+                xw = xsb[:, 2 * pair + rr, :].bitcast(F32)
+                for u in range(2):
+                    nc.tensor.transpose(xt[:, rr, u, :], xw[:, P * u : P * u + P], ident[:])
+            nc.vector.tensor_copy(
+                out=xg[:].bitcast(F32)[:, 2 * pair : 2 * pair + 2],
+                in_=xt[:].rearrange("p r u m -> p r m u"),
+            )
+
+        def quant_x(c):
+            nc.vector.quantize_mx(
+                out=xc[:, 512 * c : 512 * c + 512].bitcast(FP8X4),
+                scales=xs[:, 512 * c : 512 * c + 512],
+                in_=xg[:, 4 * c : 4 * c + 4].rearrange("p r m t -> p (r m t)"),
+            )
+
+        def gate(z, k):
+            nc.scalar.activation(out=z[:, k], in_=z[:, k], func=ACT.Sigmoid)
+
+        def eff(e, z, wview, k):
+            nc.vector.tensor_tensor(
+                out=e[:, k], in0=wview.rearrange("p t h -> p h t"),
+                in1=z[:, k].rearrange("p t h -> p h t"), op=ALU.mult,
+            )
+
+        def quant_w(e, cw, sw, k):
+            nc.vector.quantize_mx(
+                out=cw[:, CH * k : CH * k + CH].bitcast(FP8X4),
+                scales=sw[:, CH * k : CH * k + CH],
+                in_=e[:, k].rearrange("p h t -> p (h t)"),
+            )
+
+        def len2_v(q):
+            if q in ABS2:
+                abs_v((2, q))
+            else:
+                max_v((2, q), [2 * q, 2 * q + 1])
+
+        for q in range(4):
+            abs_s((1, q), hpb, nip, [q], H)
+        for q in ABS2:
+            abs_s((2, q), opb, nhp, [2 * q, 2 * q + 1], O)
+        len2_v(0)
+        abs_v((1, 0))
+        clamp(wc1, w1sb)
+        abs_v((1, 1))
+        len2_v(1)
+        abs_v((1, 2))
+        abs_v((1, 3))
+        clamp(wc2, w2sb)
+        ln_width(z1, wc1, 0, 4)
+        for q in range(4):
+            ln_len((1, q), 1.0)
+        len2_v(2)
+        zed1(0)
+        zed1(1)
+        len2_v(3)
+        ln_width(z2, wc2, 0, 2)
+        ln_width(z2, wc2, 1, 2)
+        for q in range(4):
+            ln_len((2, q), 1.0 if q in ABS2 else 2.0)
+        zed1(2)
+        zed1(3)
+        transposes(0)
+        transposes(1)
+        quant_x(0)
+        b1f = const.tile([P, 8], F32)
+        nc.vector.tensor_copy(out=b1f[:], in_=b1sb[:])
+        for q in range(4):
+            zed2(q)
+
+        e1 = w8.tile([P, 4, CH, 4], BF16, name="e1", tag="w8", align_bytes=64)
+        e2 = w8.tile([P, 4, CH, 4], BF16, name="e2", tag="w8", align_bytes=64)
+        for k in range(4):
+            gate(z1, k)
+            eff(e1, z1, w1sb[:, :, CH * k : CH * k + CH], k)
+            if k > 0:
+                quant_w(e1, c1, s1, k - 1)
+        for k in range(4):
+            gate(z2, k)
+        transposes(2)
+        quant_w(e1, c1, s1, 3)
+        transposes(3)
+        quant_x(1)
+
+        def eff2(k):
+            g, oh = k // 2, k % 2
+            eff(e2, z2, w2sb[:, 4 * g : 4 * g + 4, CH * oh : CH * oh + CH], k)
+
+        ov = out.rearrange("(m r) o -> m r o", r=16)
+        hid = {}
+
+        def l1_mm(c, mts):
+            if c not in hid:
+                hc = hp.tile([P, 8, 512], BF16, name="hc")
+                gc = hp.tile([P, 2, 512, 4], BF16, name="gc", align_bytes=64)
+                cc = hq.tile([P, 2, 512], U32, name="cc", align_bytes=64)
+                sc = hq.tile([P, 2, 512], U8, name="sc", align_bytes=64)
+                hid[c] = (hc, gc, cc, sc)
+            hc = hid[c][0]
+            for mt in mts:
+                ps = psa.tile([P, 512], F32, name="ps")
+                nc.tensor.matmul_mx(
+                    out=ps[:],
+                    lhsT=c1[:, P * mt : P * mt + P].bitcast(FP8X4),
+                    lhsT_scale=s1[:, P * mt : P * mt + P],
+                    rhs=xc[:, 512 * c : 512 * c + 512].bitcast(FP8X4),
+                    rhs_scale=xs[:, 512 * c : 512 * c + 512],
+                    start=True, stop=True,
+                )
+                nc.scalar.activation(
+                    out=hc[:, mt, :], in_=ps[:], func=ACT.Sigmoid, bias=b1f[:, mt : mt + 1], scale=1.0
+                )
+
+        def regroup(c, g):
+            hc, gc = hid[c][0], hid[c][1]
+            nc.vector.tensor_copy(
+                out=gc[:, g].rearrange("p (c i) t -> p c t i", i=4),
+                in_=hc[:, 4 * g : 4 * g + 4, :].rearrange("p t (c i) -> p c t i", i=4),
+            )
+
+        def quant_h(c, g):
+            gc, cc, sc = hid[c][1], hid[c][2], hid[c][3]
+            nc.vector.quantize_mx(
+                out=cc[:, g].bitcast(FP8X4), scales=sc[:, g], in_=gc[:, g].rearrange("p b t -> p (b t)")
+            )
+
+        outs = {}
+
+        def l2_mm(c, rr):
+            cc, sc = hid[c][2], hid[c][3]
+            ps2 = psb.tile([P, 512], F32, name="ps2")
+            for g in range(2):
+                nc.tensor.matmul_mx(
+                    out=ps2[:],
+                    lhsT=cc[:, g, P * rr : P * rr + P].bitcast(FP8X4),
+                    lhsT_scale=sc[:, g, P * rr : P * rr + P],
+                    rhs=c2[:, 512 * g : 512 * g + 512].bitcast(FP8X4),
+                    rhs_scale=s2[:, 512 * g : 512 * g + 512],
+                    start=(g == 0), stop=(g == 1),
+                )
+            ot = op.tile([P, 512], F32, name="ot")
+            outs[(c, rr)] = ot
+            nc.vector.tensor_tensor(out=ot[:], in0=ps2[:], in1=b2b[:], op=ALU.add)
+
+        def l2_out(c, rr):
+            ot = outs[(c, rr)]
+            nc.scalar.activation(out=ot[:], in_=ot[:], func=ACT.Sigmoid)
+            nc.sync.dma_start(out=ov[:, 4 * c + rr, :], in_=ot[:])
+
+        l1_mm(0, range(0, 8))
+        eff2(0)
+        eff2(1)
+        quant_w(e2, c2, s2, 0)
+        regroup(0, 0)
+        quant_w(e2, c2, s2, 1)
+        transposes(4)
+        quant_h(0, 0)
+        transposes(5)
+        regroup(0, 1)
+        quant_x(2)
+        l1_mm(1, range(0, 8))
+        eff2(2)
+        quant_h(0, 1)
+        eff2(3)
+        quant_w(e2, c2, s2, 2)
+        regroup(1, 0)
+        quant_w(e2, c2, s2, 3)
+        transposes(6)
+        quant_h(1, 0)
+        transposes(7)
+        regroup(1, 1)
+        quant_x(3)
+        l1_mm(2, range(0, 8))
+        for rr in range(4):
+            l2_mm(0, rr)
+        quant_h(1, 1)
+        regroup(2, 0)
+        for rr in range(4):
+            l2_out(0, rr)
+        l1_mm(3, range(0, 8))
+        l2_mm(1, 0)
+        quant_h(2, 0)
+        regroup(2, 1)
+        l2_mm(1, 1)
+        quant_h(2, 1)
+        l2_mm(1, 2)
+        l2_mm(1, 3)
+        regroup(3, 0)
+        for rr in range(4):
+            l2_out(1, rr)
+        l2_mm(2, 0)
+        quant_h(3, 0)
+        l2_mm(2, 1)
+        regroup(3, 1)
+        l2_mm(2, 2)
+        quant_h(3, 1)
+        l2_mm(2, 3)
+        for rr in range(4):
+            l2_out(2, rr)
+        for rr in range(4):
+            l2_mm(3, rr)
+            l2_out(3, rr)

@@ -29,32 +29,27 @@ def tile_physicalneuralnetwork_kernel(
     with ExitStack() as ctx:
         const = ctx.enter_context(tc.tile_pool(name="const", bufs=1))
         w8 = ctx.enter_context(tc.tile_pool(name="w8", bufs=2))
-        a1p = ctx.enter_context(tc.tile_pool(name="a1p", bufs=8))
+        a1p = ctx.enter_context(tc.tile_pool(name="a1p", bufs=7))
         a2p = ctx.enter_context(tc.tile_pool(name="a2p", bufs=3))
         hp = ctx.enter_context(tc.tile_pool(name="hp", bufs=2))
         hq = ctx.enter_context(tc.tile_pool(name="hq", bufs=3))
-        op = ctx.enter_context(tc.tile_pool(name="op", bufs=4))
+        op = ctx.enter_context(tc.tile_pool(name="op", bufs=7))
         psx = ctx.enter_context(tc.psum_pool(name="psx", bufs=2))
-        psa = ctx.enter_context(tc.psum_pool(name="psa", bufs=4))
-        psb = ctx.enter_context(tc.psum_pool(name="psb", bufs=2))
         ctx.enter_context(nc.allow_non_contiguous_dma(reason="small per-partition vectors"))
 
         ipos = const.tile([P, 2, 4], BF16)
         nc.sync.dma_start(
             out=ipos[:], in_=input_positions.rearrange("(u p e) c -> p u (e c)", u=2, e=2)
         )
-        hpb = const.tile([P, H, 2], BF16)
-        nc.sync.dma_start(
-            out=hpb[:].rearrange("p h c -> p (h c)"),
-            in_=hidden_positions.rearrange("h c -> (h c)").partition_broadcast(P),
-        )
+        row1 = const.tile([P, 2 * H], BF16)
+        nc.vector.memset(row1[:], 0.0)
+        nc.sync.dma_start(out=row1[0:1, :], in_=hidden_positions.rearrange("(a h) c -> a (h c)", a=1))
         hpos = const.tile([P, 8, 2], BF16)
         nc.sync.dma_start(out=hpos[:], in_=hidden_positions.rearrange("(a p) c -> p a c", p=P))
-        opb = const.tile([P, O, 2], BF16)
-        nc.sync.dma_start(
-            out=opb[:].rearrange("p h c -> p (h c)"),
-            in_=output_positions.rearrange("h c -> (h c)").partition_broadcast(P),
-        )
+        row2 = const.tile([P, 3 * O], BF16)
+        nc.vector.memset(row2[:], 0.0)
+        nc.sync.dma_start(out=row2[0:1, 0 : 2 * O], in_=output_positions.rearrange("(a h) c -> a (h c)", a=1))
+        nc.sync.dma_start(out=row2[0:1, 2 * O : 3 * O], in_=b2.rearrange("(a o) -> a o", a=1))
         w1sb = const.tile([P, 4, H], BF16)
         nc.sync.dma_start(
             out=w1sb[:].rearrange("p (u e) h -> p u (e h)", u=2),
@@ -69,179 +64,203 @@ def tile_physicalneuralnetwork_kernel(
             nc.sync.dma_start(out=xsb[:, 4 * c : 4 * c + 4, :], in_=xv[:, 4 * c : 4 * c + 4, :])
         b1sb = const.tile([P, 8], BF16)
         nc.sync.dma_start(out=b1sb[:], in_=b1.rearrange("(a p) -> p a", p=P))
-        b2b = const.tile([P, O], BF16)
-        nc.sync.dma_start(out=b2b[:], in_=b2.partition_broadcast(P))
 
         ident = const.tile([P, P], F32)
         make_identity(nc, ident[:])
 
-        eps = const.tile([P, 1], F32)
-        nc.vector.memset(eps[:], EPS)
-        one = const.tile([P, 1], F32)
-        nc.vector.memset(one[:], 1.0)
-        warm = const.tile([P, 1], F32)
-        nc.scalar.activation(out=warm[:], in_=one[:], func=ACT.Ln)
-        nip = const.tile([P, 8], F32)
-        nc.vector.tensor_scalar_mul(out=nip[:], in0=ipos[:].rearrange("p u k -> p (u k)"), scalar1=-1.0)
-        hpf = const.tile([P, 8, 2], F32)
-        nc.vector.tensor_copy(out=hpf[:], in_=hpos[:])
-        nhp = const.tile([P, 16], F32)
-        nc.vector.tensor_scalar_mul(out=nhp[:], in0=hpos[:].rearrange("p a c -> p (a c)"), scalar1=-1.0)
-        nhs = const.tile([P, 8], F32)
-        nc.vector.tensor_tensor(out=nhs[:], in0=hpf[:, :, 0], in1=hpf[:, :, 1], op=ALU.add)
-        nc.vector.tensor_scalar_mul(out=nhs[:], in0=nhs[:], scalar1=-0.5)
-        nos = const.tile([P, O], F32)
-        nc.vector.tensor_tensor(out=nos[:], in0=opb[:, :, 0], in1=opb[:, :, 1], op=ALU.add)
-        nc.vector.tensor_scalar_mul(out=nos[:], in0=nos[:], scalar1=-0.5)
+        with tc.psum_pool(name="psp", bufs=1) as psp:
+            ones = const.tile([P, P], BF16)
+            nc.vector.memset(ones[:], 1.0)
 
-        xg = const.tile([P, 16, P, 4], BF16, align_bytes=64)
-        xc = const.tile([P, B], U32, align_bytes=64)
-        xs = const.tile([P, B], U8, align_bytes=64)
-        z1 = const.tile([P, 4, 4, CH], F32)
-        z2 = const.tile([P, 4, 4, CH], F32)
-        c1 = const.tile([P, 4 * CH], U32, align_bytes=64)
-        s1 = const.tile([P, 4 * CH], U8, align_bytes=64)
-        c2 = const.tile([P, 4 * CH], U32, align_bytes=64)
-        s2 = const.tile([P, 4 * CH], U8, align_bytes=64)
-        wc1 = w8.tile([P, 4, H], BF16, name="wc1", tag="w8", align_bytes=64)
-        wc2 = w8.tile([P, 8, O], BF16, name="wc2", tag="w8", align_bytes=64)
-        lt = {}
+            def spread(pool, src, name, tag):
+                t = pool.tile([P, 512], F32, name=name, tag=tag)
+                nc.tensor.matmul(out=t[:], lhsT=ones[:], rhs=src, start=True, stop=True)
+                return t
 
-        def clamp(wc, wsb):
-            nc.vector.tensor_scalar(
-                out=wc[:], in0=wsb[:], scalar1=-3.0, scalar2=3.0, op0=ALU.max, op1=ALU.min
+            hxp = [spread(psp, row1[:, 1024 * k : 1024 * k + 1024 : 2], "hx%d" % k, "hx%d" % k) for k in range(2)]
+            hyp = [spread(psp, row1[:, 1024 * k + 1 : 1024 * k + 1024 : 2], "hy%d" % k, "hy%d" % k) for k in range(2)]
+            oxp = [spread(psp, row2[:, 0:1024:2], "ox", "ox")]
+            oyp = [spread(psp, row2[:, 1:1024:2], "oy", "oy")]
+            b2p = spread(psx, row2[:, 1024:1536], "b2p", "xt")
+
+            eps = const.tile([P, 1], F32)
+            nc.vector.memset(eps[:], EPS)
+            one = const.tile([P, 1], F32)
+            nc.vector.memset(one[:], 1.0)
+            warm = const.tile([P, 1], F32)
+            nc.scalar.activation(out=warm[:], in_=one[:], func=ACT.Ln)
+            nip = const.tile([P, 8], F32)
+            nc.vector.tensor_scalar_mul(out=nip[:], in0=ipos[:].rearrange("p u k -> p (u k)"), scalar1=-1.0)
+            hpf = const.tile([P, 8, 2], F32)
+            nc.vector.tensor_copy(out=hpf[:], in_=hpos[:])
+            nhp = const.tile([P, 16], F32)
+            nc.vector.tensor_scalar_mul(out=nhp[:], in0=hpos[:].rearrange("p a c -> p (a c)"), scalar1=-1.0)
+            nhs = const.tile([P, 8], F32)
+            nc.vector.tensor_tensor(out=nhs[:], in0=hpf[:, :, 0], in1=hpf[:, :, 1], op=ALU.add)
+            nc.vector.tensor_scalar_mul(out=nhs[:], in0=nhs[:], scalar1=-0.5)
+            nos = const.tile([P, O], F32)
+            nc.vector.tensor_scalar_mul(out=nos[:], in0=oxp[0][:], scalar1=-0.5)
+            nc.vector.scalar_tensor_tensor(
+                out=nos[:], in0=oyp[0][:], scalar=-0.5, in1=nos[:], op0=ALU.mult, op1=ALU.add
             )
+            b2b = const.tile([P, O], F32)
+            nc.vector.tensor_copy(out=b2b[:], in_=b2p[:])
 
-        def abs_s(key, posb, npos, rows, n):
-            a1 = a1p.tile([P, 1024], F32, name="a1")
-            a2 = a2p.tile([P, 1024], F32, name="a2")
-            lt[key] = (a1, a2)
-            for k, j in enumerate(rows):
-                nc.scalar.activation(
-                    out=a1[:, k * n : (k + 1) * n], in_=posb[:, :, 0], func=ACT.Abs,
-                    bias=npos[:, 2 * j : 2 * j + 1], scale=1.0,
-                )
-                nc.scalar.activation(
-                    out=a2[:, k * n : (k + 1) * n], in_=posb[:, :, 1], func=ACT.Abs,
-                    bias=npos[:, 2 * j + 1 : 2 * j + 2], scale=1.0,
-                )
+            xg = const.tile([P, 16, P, 4], BF16, align_bytes=64)
+            xc = const.tile([P, B], U32, align_bytes=64)
+            xs = const.tile([P, B], U8, align_bytes=64)
+            z1 = const.tile([P, 4, 4, CH], F32)
+            z2 = const.tile([P, 4, 4, CH], F32)
+            c1 = const.tile([P, 4 * CH], U32, align_bytes=64)
+            s1 = const.tile([P, 4 * CH], U8, align_bytes=64)
+            c2 = const.tile([P, 4 * CH], U32, align_bytes=64)
+            s2 = const.tile([P, 4 * CH], U8, align_bytes=64)
+            wc1 = w8.tile([P, 4, H], BF16, name="wc1", tag="w8", align_bytes=64)
+            wc2 = w8.tile([P, 8, O], BF16, name="wc2", tag="w8", align_bytes=64)
+            lt = {}
 
-        def abs_v(key):
-            a1, a2 = lt[key]
-            nc.vector.tensor_tensor(out=a1[:], in0=a1[:], in1=a2[:], op=ALU.add)
-
-        def max_v(key, rows):
-            a1 = a1p.tile([P, 1024], F32, name="a1")
-            lt[key] = (a1, None)
-            for k, j in enumerate(rows):
-                sl = a1[:, k * O : (k + 1) * O]
-                nc.vector.scalar_tensor_tensor(
-                    out=sl, in0=opb[:, :, 0], scalar=hpf[:, j, 0:1], in1=nos[:], op0=ALU.max, op1=ALU.add
-                )
-                nc.vector.scalar_tensor_tensor(
-                    out=sl, in0=opb[:, :, 1], scalar=hpf[:, j, 1:2], in1=sl, op0=ALU.max, op1=ALU.add
-                )
+            def clamp(wc, wsb):
                 nc.vector.tensor_scalar(
-                    out=sl, in0=sl, scalar1=nhs[:, j : j + 1], scalar2=0.0, op0=ALU.add, op1=ALU.max
+                    out=wc[:], in0=wsb[:], scalar1=-3.0, scalar2=3.0, op0=ALU.max, op1=ALU.min
                 )
 
-        def ln_width(z, wc, g, kper):
-            nc.scalar.activation(
-                out=z[:, g * kper : (g + 1) * kper],
-                in_=wc[:, 4 * g : 4 * g + 4, :].rearrange("p t (k h) -> p k t h", h=CH),
-                func=ACT.Ln, bias=one[:], scale=WA / WB,
-            )
+            def abs_s(key, px, py, npos, rows):
+                a1 = a1p.tile([P, 1024], F32, name="a1")
+                a2 = a2p.tile([P, 1024], F32, name="a2")
+                lt[key] = (a1, a2)
+                col = 0
+                for j in rows:
+                    for k in range(len(px)):
+                        nc.scalar.activation(
+                            out=a1[:, col : col + 512], in_=px[k][:], func=ACT.Abs,
+                            bias=npos[:, 2 * j : 2 * j + 1], scale=1.0,
+                        )
+                        nc.scalar.activation(
+                            out=a2[:, col : col + 512], in_=py[k][:], func=ACT.Abs,
+                            bias=npos[:, 2 * j + 1 : 2 * j + 2], scale=1.0,
+                        )
+                        col += 512
 
-        def ln_len(key, factor):
-            a1 = lt[key][0]
-            nc.scalar.activation(out=a1[:], in_=a1[:], func=ACT.Ln, bias=eps[:], scale=factor * RHO / WB)
+            def abs_v(key):
+                a1, a2 = lt[key]
+                nc.vector.tensor_tensor(out=a1[:], in0=a1[:], in1=a2[:], op=ALU.add)
 
-        def zed1(q):
-            nc.vector.tensor_tensor(
-                out=z1[:, :, q, :], in0=z1[:, :, q, :],
-                in1=lt[(1, q)][0][:].rearrange("p (k h) -> p k h", h=CH), op=ALU.subtract,
-            )
+            def max_v(key, rows):
+                a1 = a1p.tile([P, 1024], F32, name="a1")
+                lt[key] = (a1, None)
+                for k, j in enumerate(rows):
+                    sl = a1[:, k * O : (k + 1) * O]
+                    nc.vector.scalar_tensor_tensor(
+                        out=sl, in0=oxp[0][:], scalar=hpf[:, j, 0:1], in1=nos[:], op0=ALU.max, op1=ALU.add
+                    )
+                    nc.vector.scalar_tensor_tensor(
+                        out=sl, in0=oyp[0][:], scalar=hpf[:, j, 1:2], in1=sl, op0=ALU.max, op1=ALU.add
+                    )
+                    nc.vector.tensor_scalar(
+                        out=sl, in0=sl, scalar1=nhs[:, j : j + 1], scalar2=0.0, op0=ALU.add, op1=ALU.max
+                    )
 
-        def zed2(q):
-            g, t0 = q // 2, 2 * (q % 2)
-            zv = z2[:, 2 * g : 2 * g + 2, t0 : t0 + 2, :]
-            nc.vector.tensor_tensor(
-                out=zv, in0=zv, in1=lt[(2, q)][0][:].rearrange("p (t k h) -> p k t h", t=2, h=CH),
-                op=ALU.subtract,
-            )
+            def ln_width(z, wc, g, kper):
+                nc.scalar.activation(
+                    out=z[:, g * kper : (g + 1) * kper],
+                    in_=wc[:, 4 * g : 4 * g + 4, :].rearrange("p t (k h) -> p k t h", h=CH),
+                    func=ACT.Ln, bias=one[:], scale=WA / WB,
+                )
 
-        def transposes(pair):
-            xt = psx.tile([P, 2, 2, P], F32, name="xt")
-            for rr in range(2):
-                xw = xsb[:, 2 * pair + rr, :].bitcast(F32)
-                for u in range(2):
-                    nc.tensor.transpose(xt[:, rr, u, :], xw[:, P * u : P * u + P], ident[:])
-            nc.vector.tensor_copy(
-                out=xg[:].bitcast(F32)[:, 2 * pair : 2 * pair + 2],
-                in_=xt[:].rearrange("p r u m -> p r m u"),
-            )
+            def ln_len(key, factor):
+                a1 = lt[key][0]
+                nc.scalar.activation(out=a1[:], in_=a1[:], func=ACT.Ln, bias=eps[:], scale=factor * RHO / WB)
 
-        def quant_x(c):
-            nc.vector.quantize_mx(
-                out=xc[:, 512 * c : 512 * c + 512].bitcast(FP8X4),
-                scales=xs[:, 512 * c : 512 * c + 512],
-                in_=xg[:, 4 * c : 4 * c + 4].rearrange("p r m t -> p (r m t)"),
-            )
+            def zed1(q):
+                nc.vector.tensor_tensor(
+                    out=z1[:, :, q, :], in0=z1[:, :, q, :],
+                    in1=lt[(1, q)][0][:].rearrange("p (k h) -> p k h", h=CH), op=ALU.subtract,
+                )
 
-        def gate(z, k):
-            nc.scalar.activation(out=z[:, k], in_=z[:, k], func=ACT.Sigmoid)
+            def zed2(q):
+                g, t0 = q // 2, 2 * (q % 2)
+                zv = z2[:, 2 * g : 2 * g + 2, t0 : t0 + 2, :]
+                nc.vector.tensor_tensor(
+                    out=zv, in0=zv, in1=lt[(2, q)][0][:].rearrange("p (t k h) -> p k t h", t=2, h=CH),
+                    op=ALU.subtract,
+                )
 
-        def eff(e, z, wview, k):
-            nc.vector.tensor_tensor(
-                out=e[:, k], in0=wview.rearrange("p t h -> p h t"),
-                in1=z[:, k].rearrange("p t h -> p h t"), op=ALU.mult,
-            )
+            def transposes(pair):
+                xt = psx.tile([P, 2, 2, P], F32, name="xt")
+                for rr in range(2):
+                    xw = xsb[:, 2 * pair + rr, :].bitcast(F32)
+                    for u in range(2):
+                        nc.tensor.transpose(xt[:, rr, u, :], xw[:, P * u : P * u + P], ident[:])
+                nc.vector.tensor_copy(
+                    out=xg[:].bitcast(F32)[:, 2 * pair : 2 * pair + 2],
+                    in_=xt[:].rearrange("p r u m -> p r m u"),
+                )
 
-        def quant_w(e, cw, sw, k):
-            nc.vector.quantize_mx(
-                out=cw[:, CH * k : CH * k + CH].bitcast(FP8X4),
-                scales=sw[:, CH * k : CH * k + CH],
-                in_=e[:, k].rearrange("p h t -> p (h t)"),
-            )
+            def quant_x(c):
+                nc.vector.quantize_mx(
+                    out=xc[:, 512 * c : 512 * c + 512].bitcast(FP8X4),
+                    scales=xs[:, 512 * c : 512 * c + 512],
+                    in_=xg[:, 4 * c : 4 * c + 4].rearrange("p r m t -> p (r m t)"),
+                )
 
-        def len2_v(q):
-            if q in ABS2:
-                abs_v((2, q))
-            else:
-                max_v((2, q), [2 * q, 2 * q + 1])
+            def gate(z, k):
+                nc.scalar.activation(out=z[:, k], in_=z[:, k], func=ACT.Sigmoid)
 
-        for q in range(4):
-            abs_s((1, q), hpb, nip, [q], H)
-        for q in ABS2:
-            abs_s((2, q), opb, nhp, [2 * q, 2 * q + 1], O)
-        len2_v(0)
-        abs_v((1, 0))
-        clamp(wc1, w1sb)
-        abs_v((1, 1))
-        len2_v(1)
-        abs_v((1, 2))
-        abs_v((1, 3))
-        clamp(wc2, w2sb)
-        ln_width(z1, wc1, 0, 4)
-        for q in range(4):
-            ln_len((1, q), 1.0)
-        len2_v(2)
-        zed1(0)
-        zed1(1)
-        len2_v(3)
-        ln_width(z2, wc2, 0, 2)
-        ln_width(z2, wc2, 1, 2)
-        for q in range(4):
-            ln_len((2, q), 1.0 if q in ABS2 else 2.0)
-        zed1(2)
-        zed1(3)
-        transposes(0)
-        transposes(1)
-        quant_x(0)
-        b1f = const.tile([P, 8], F32)
-        nc.vector.tensor_copy(out=b1f[:], in_=b1sb[:])
-        for q in range(4):
-            zed2(q)
+            def eff(e, z, wview, k):
+                nc.vector.tensor_tensor(
+                    out=e[:, k].rearrange("p (c i) t -> p c t i", i=4),
+                    in0=wview.rearrange("p t (c i) -> p c t i", i=4),
+                    in1=z[:, k].rearrange("p t (c i) -> p c t i", i=4), op=ALU.mult,
+                )
+
+            def quant_w(e, cw, sw, k):
+                nc.vector.quantize_mx(
+                    out=cw[:, CH * k : CH * k + CH].bitcast(FP8X4),
+                    scales=sw[:, CH * k : CH * k + CH],
+                    in_=e[:, k].rearrange("p h t -> p (h t)"),
+                )
+
+            def len2_v(q):
+                if q in ABS2:
+                    abs_v((2, q))
+                else:
+                    max_v((2, q), [2 * q, 2 * q + 1])
+
+            for q in range(4):
+                abs_s((1, q), hxp, hyp, nip, [q])
+            for q in ABS2:
+                abs_s((2, q), oxp, oyp, nhp, [2 * q, 2 * q + 1])
+            len2_v(0)
+            abs_v((1, 0))
+            clamp(wc1, w1sb)
+            abs_v((1, 1))
+            len2_v(1)
+            abs_v((1, 2))
+            abs_v((1, 3))
+            clamp(wc2, w2sb)
+            ln_width(z1, wc1, 0, 4)
+            for q in range(4):
+                ln_len((1, q), 1.0)
+            len2_v(2)
+            zed1(0)
+            zed1(1)
+            len2_v(3)
+            ln_width(z2, wc2, 0, 2)
+            ln_width(z2, wc2, 1, 2)
+            for q in range(4):
+                ln_len((2, q), 1.0 if q in ABS2 else 2.0)
+            zed1(2)
+            zed1(3)
+            transposes(0)
+            transposes(1)
+            quant_x(0)
+            b1f = const.tile([P, 8], F32)
+            nc.vector.tensor_copy(out=b1f[:], in_=b1sb[:])
+            for q in range(4):
+                zed2(q)
+
+        psa = ctx.enter_context(tc.psum_pool(name="psa", bufs=4))
+        psb = ctx.enter_context(tc.psum_pool(name="psb", bufs=2))
 
         e1 = w8.tile([P, 4, CH, 4], BF16, name="e1", tag="w8", align_bytes=64)
         e2 = w8.tile([P, 4, CH, 4], BF16, name="e2", tag="w8", align_bytes=64)

@@ -19,7 +19,7 @@ WA = (5.0 - 0.09) / 6.0
 WB = 0.09 + (5.0 - 0.09) / 2.0
 EPS = 1e-18
 CH = 256
-ABS2 = (3,)
+SCALAR_PAIRS = (7,)
 
 
 def tile_physicalneuralnetwork_kernel(
@@ -29,21 +29,16 @@ def tile_physicalneuralnetwork_kernel(
     with ExitStack() as ctx:
         const = ctx.enter_context(tc.tile_pool(name="const", bufs=1))
         w8 = ctx.enter_context(tc.tile_pool(name="w8", bufs=2))
-        a1p = ctx.enter_context(tc.tile_pool(name="a1p", bufs=7))
-        a2p = ctx.enter_context(tc.tile_pool(name="a2p", bufs=3))
+        atp = ctx.enter_context(tc.tile_pool(name="atp", bufs=3))
         hp = ctx.enter_context(tc.tile_pool(name="hp", bufs=2))
         hq = ctx.enter_context(tc.tile_pool(name="hq", bufs=3))
-        op = ctx.enter_context(tc.tile_pool(name="op", bufs=7))
+        op = ctx.enter_context(tc.tile_pool(name="op", bufs=6))
         psx = ctx.enter_context(tc.psum_pool(name="psx", bufs=2))
         ctx.enter_context(nc.allow_non_contiguous_dma(reason="small per-partition vectors"))
 
-        ipos = const.tile([P, 2, 4], BF16)
-        nc.sync.dma_start(
-            out=ipos[:], in_=input_positions.rearrange("(u p e) c -> p u (e c)", u=2, e=2)
-        )
-        row1 = const.tile([P, 2 * H], BF16)
-        nc.vector.memset(row1[:], 0.0)
-        nc.sync.dma_start(out=row1[0:1, :], in_=hidden_positions.rearrange("(a h) c -> a (h c)", a=1))
+        rowi = const.tile([P, 2 * I], BF16)
+        nc.vector.memset(rowi[:], 0.0)
+        nc.sync.dma_start(out=rowi[0:1, :], in_=input_positions.rearrange("(a h) c -> a (h c)", a=1))
         hpos = const.tile([P, 8, 2], BF16)
         nc.sync.dma_start(out=hpos[:], in_=hidden_positions.rearrange("(a p) c -> p a c", p=P))
         row2 = const.tile([P, 3 * O], BF16)
@@ -68,7 +63,70 @@ def tile_physicalneuralnetwork_kernel(
         ident = const.tile([P, P], F32)
         make_identity(nc, ident[:])
 
-        with tc.psum_pool(name="psp", bufs=1) as psp:
+        xg = const.tile([P, 16, P, 4], BF16, align_bytes=64)
+        xc = const.tile([P, B], U32, align_bytes=64)
+        xs = const.tile([P, B], U8, align_bytes=64)
+        z1 = const.tile([P, 4, 4, CH], F32)
+        z2 = const.tile([P, 4, 4, CH], F32)
+        ll1 = const.tile([P, 4, H], F32)
+        ll2 = const.tile([P, 8, O], F32)
+        c1 = const.tile([P, 4 * CH], U32, align_bytes=64)
+        s1 = const.tile([P, 4 * CH], U8, align_bytes=64)
+        c2 = const.tile([P, 4 * CH], U32, align_bytes=64)
+        s2 = const.tile([P, 4 * CH], U8, align_bytes=64)
+        wc1 = w8.tile([P, 4, H], BF16, name="wc1", tag="w8", align_bytes=64)
+        wc2 = w8.tile([P, 8, O], BF16, name="wc2", tag="w8", align_bytes=64)
+
+        def clamp(wc, wsb):
+            nc.vector.tensor_scalar(
+                out=wc[:], in0=wsb[:], scalar1=-3.0, scalar2=3.0, op0=ALU.max, op1=ALU.min
+            )
+
+        def ln_width(z, wc, g, kper):
+            nc.scalar.activation(
+                out=z[:, g * kper : (g + 1) * kper],
+                in_=wc[:, 4 * g : 4 * g + 4, :].rearrange("p t (k h) -> p k t h", h=CH),
+                func=ACT.Ln, bias=one[:], scale=WA / WB,
+            )
+
+        def transposes(pair):
+            xt = psx.tile([P, 2, 2, P], F32, name="xt")
+            for rr in range(2):
+                xw = xsb[:, 2 * pair + rr, :].bitcast(F32)
+                for u in range(2):
+                    nc.tensor.transpose(xt[:, rr, u, :], xw[:, P * u : P * u + P], ident[:])
+            dst = xg[:].bitcast(F32)[:, 2 * pair : 2 * pair + 2]
+            src = xt[:].rearrange("p r u m -> p r m u")
+            if pair in SCALAR_PAIRS:
+                nc.scalar.copy(out=dst, in_=src)
+            else:
+                nc.vector.tensor_copy(out=dst, in_=src)
+
+        def quant_x(c):
+            nc.vector.quantize_mx(
+                out=xc[:, 512 * c : 512 * c + 512].bitcast(FP8X4),
+                scales=xs[:, 512 * c : 512 * c + 512],
+                in_=xg[:, 4 * c : 4 * c + 4].rearrange("p r m t -> p (r m t)"),
+            )
+
+        def gate(z, k):
+            nc.scalar.activation(out=z[:, k], in_=z[:, k], func=ACT.Sigmoid)
+
+        def eff(e, z, wview, k):
+            nc.vector.tensor_tensor(
+                out=e[:, k].rearrange("p (c i) t -> p c t i", i=4),
+                in0=wview.rearrange("p t (c i) -> p c t i", i=4),
+                in1=z[:, k].rearrange("p t (c i) -> p c t i", i=4), op=ALU.mult,
+            )
+
+        def quant_w(e, cw, sw, k):
+            nc.vector.quantize_mx(
+                out=cw[:, CH * k : CH * k + CH].bitcast(FP8X4),
+                scales=sw[:, CH * k : CH * k + CH],
+                in_=e[:, k].rearrange("p h t -> p (h t)"),
+            )
+
+        with tc.psum_pool(name="psp", bufs=1) as psp, tc.psum_pool(name="psl", bufs=2) as psl:
             ones = const.tile([P, P], BF16)
             nc.vector.memset(ones[:], 1.0)
 
@@ -77,10 +135,11 @@ def tile_physicalneuralnetwork_kernel(
                 nc.tensor.matmul(out=t[:], lhsT=ones[:], rhs=src, start=True, stop=True)
                 return t
 
-            hxp = [spread(psp, row1[:, 1024 * k : 1024 * k + 1024 : 2], "hx%d" % k, "hx%d" % k) for k in range(2)]
-            hyp = [spread(psp, row1[:, 1024 * k + 1 : 1024 * k + 1024 : 2], "hy%d" % k, "hy%d" % k) for k in range(2)]
-            oxp = [spread(psp, row2[:, 0:1024:2], "ox", "ox")]
-            oyp = [spread(psp, row2[:, 1:1024:2], "oy", "oy")]
+            iv = rowi[:].rearrange("k (u p e c) -> k c u e p", u=2, p=P, e=2, c=2)
+            ixp = spread(psp, iv[:, 0], "ix", "ix")
+            iyp = spread(psp, iv[:, 1], "iy", "iy")
+            oxp = spread(psp, row2[:, 0:1024:2], "ox", "ox")
+            oyp = spread(psp, row2[:, 1:1024:2], "oy", "oy")
             b2p = spread(psx, row2[:, 1024:1536], "b2p", "xt")
 
             eps = const.tile([P, 1], F32)
@@ -89,175 +148,96 @@ def tile_physicalneuralnetwork_kernel(
             nc.vector.memset(one[:], 1.0)
             warm = const.tile([P, 1], F32)
             nc.scalar.activation(out=warm[:], in_=one[:], func=ACT.Ln)
-            nip = const.tile([P, 8], F32)
-            nc.vector.tensor_scalar_mul(out=nip[:], in0=ipos[:].rearrange("p u k -> p (u k)"), scalar1=-1.0)
-            hpf = const.tile([P, 8, 2], F32)
-            nc.vector.tensor_copy(out=hpf[:], in_=hpos[:])
             nhp = const.tile([P, 16], F32)
             nc.vector.tensor_scalar_mul(out=nhp[:], in0=hpos[:].rearrange("p a c -> p (a c)"), scalar1=-1.0)
+            hpf = const.tile([P, 8, 2], F32)
+            nc.vector.tensor_copy(out=hpf[:], in_=hpos[:])
             nhs = const.tile([P, 8], F32)
             nc.vector.tensor_tensor(out=nhs[:], in0=hpf[:, :, 0], in1=hpf[:, :, 1], op=ALU.add)
             nc.vector.tensor_scalar_mul(out=nhs[:], in0=nhs[:], scalar1=-0.5)
             nos = const.tile([P, O], F32)
-            nc.vector.tensor_scalar_mul(out=nos[:], in0=oxp[0][:], scalar1=-0.5)
+            nc.vector.tensor_scalar_mul(out=nos[:], in0=oxp[:], scalar1=-0.5)
             nc.vector.scalar_tensor_tensor(
-                out=nos[:], in0=oyp[0][:], scalar=-0.5, in1=nos[:], op0=ALU.mult, op1=ALU.add
+                out=nos[:], in0=oyp[:], scalar=-0.5, in1=nos[:], op0=ALU.mult, op1=ALU.add
             )
+
+            def len1(hb):
+                atx = atp.tile([P, 512], F32, name="atx")
+                aty = atp.tile([P, 512], F32, name="aty")
+                nc.scalar.activation(
+                    out=atx[:], in_=ixp[:], func=ACT.Abs, bias=nhp[:, 2 * hb : 2 * hb + 1], scale=1.0
+                )
+                nc.scalar.activation(
+                    out=aty[:], in_=iyp[:], func=ACT.Abs, bias=nhp[:, 2 * hb + 1 : 2 * hb + 2], scale=1.0
+                )
+                xl = psl.tile([P, 4, P], F32, name="xl")
+                for t in range(4):
+                    nc.tensor.matmul(
+                        out=xl[:, t, :], lhsT=atx[:, P * t : P * t + P], rhs=ident[:],
+                        is_transpose=True, start=True, stop=False,
+                    )
+                    nc.tensor.matmul(
+                        out=xl[:, t, :], lhsT=aty[:, P * t : P * t + P], rhs=ident[:],
+                        is_transpose=True, start=False, stop=True,
+                    )
+                return xl
+
+            def ln_len1(hb, xl):
+                nc.scalar.activation(
+                    out=ll1[:, :, P * hb : P * hb + P], in_=xl[:], func=ACT.Ln, bias=eps[:], scale=RHO / WB
+                )
+
+            def len2(j):
+                sl = ll2[:, j, :]
+                nc.vector.scalar_tensor_tensor(
+                    out=sl, in0=oxp[:], scalar=hpf[:, j, 0:1], in1=nos[:], op0=ALU.max, op1=ALU.add
+                )
+                nc.vector.scalar_tensor_tensor(
+                    out=sl, in0=oyp[:], scalar=hpf[:, j, 1:2], in1=sl, op0=ALU.max, op1=ALU.add
+                )
+                nc.vector.tensor_scalar(
+                    out=sl, in0=sl, scalar1=nhs[:, j : j + 1], scalar2=0.0, op0=ALU.add, op1=ALU.max
+                )
+
+            xls = {}
+            xls[0] = len1(0)
+            len2(0)
+            len2(1)
+            clamp(wc1, w1sb)
+            for hb in range(1, 8):
+                xls[hb] = len1(hb)
+                ln_len1(hb - 1, xls[hb - 1])
+                if hb < 7:
+                    len2(hb + 1)
+            ln_len1(7, xls[7])
+            ln_width(z1, wc1, 0, 4)
+            clamp(wc2, w2sb)
             b2b = const.tile([P, O], F32)
             nc.vector.tensor_copy(out=b2b[:], in_=b2p[:])
-
-            xg = const.tile([P, 16, P, 4], BF16, align_bytes=64)
-            xc = const.tile([P, B], U32, align_bytes=64)
-            xs = const.tile([P, B], U8, align_bytes=64)
-            z1 = const.tile([P, 4, 4, CH], F32)
-            z2 = const.tile([P, 4, 4, CH], F32)
-            c1 = const.tile([P, 4 * CH], U32, align_bytes=64)
-            s1 = const.tile([P, 4 * CH], U8, align_bytes=64)
-            c2 = const.tile([P, 4 * CH], U32, align_bytes=64)
-            s2 = const.tile([P, 4 * CH], U8, align_bytes=64)
-            wc1 = w8.tile([P, 4, H], BF16, name="wc1", tag="w8", align_bytes=64)
-            wc2 = w8.tile([P, 8, O], BF16, name="wc2", tag="w8", align_bytes=64)
-            lt = {}
-
-            def clamp(wc, wsb):
-                nc.vector.tensor_scalar(
-                    out=wc[:], in0=wsb[:], scalar1=-3.0, scalar2=3.0, op0=ALU.max, op1=ALU.min
-                )
-
-            def abs_s(key, px, py, npos, rows):
-                a1 = a1p.tile([P, 1024], F32, name="a1")
-                a2 = a2p.tile([P, 1024], F32, name="a2")
-                lt[key] = (a1, a2)
-                col = 0
-                for j in rows:
-                    for k in range(len(px)):
-                        nc.scalar.activation(
-                            out=a1[:, col : col + 512], in_=px[k][:], func=ACT.Abs,
-                            bias=npos[:, 2 * j : 2 * j + 1], scale=1.0,
-                        )
-                        nc.scalar.activation(
-                            out=a2[:, col : col + 512], in_=py[k][:], func=ACT.Abs,
-                            bias=npos[:, 2 * j + 1 : 2 * j + 2], scale=1.0,
-                        )
-                        col += 512
-
-            def abs_v(key):
-                a1, a2 = lt[key]
-                nc.vector.tensor_tensor(out=a1[:], in0=a1[:], in1=a2[:], op=ALU.add)
-
-            def max_v(key, rows):
-                a1 = a1p.tile([P, 1024], F32, name="a1")
-                lt[key] = (a1, None)
-                for k, j in enumerate(rows):
-                    sl = a1[:, k * O : (k + 1) * O]
-                    nc.vector.scalar_tensor_tensor(
-                        out=sl, in0=oxp[0][:], scalar=hpf[:, j, 0:1], in1=nos[:], op0=ALU.max, op1=ALU.add
-                    )
-                    nc.vector.scalar_tensor_tensor(
-                        out=sl, in0=oyp[0][:], scalar=hpf[:, j, 1:2], in1=sl, op0=ALU.max, op1=ALU.add
-                    )
-                    nc.vector.tensor_scalar(
-                        out=sl, in0=sl, scalar1=nhs[:, j : j + 1], scalar2=0.0, op0=ALU.add, op1=ALU.max
-                    )
-
-            def ln_width(z, wc, g, kper):
-                nc.scalar.activation(
-                    out=z[:, g * kper : (g + 1) * kper],
-                    in_=wc[:, 4 * g : 4 * g + 4, :].rearrange("p t (k h) -> p k t h", h=CH),
-                    func=ACT.Ln, bias=one[:], scale=WA / WB,
-                )
-
-            def ln_len(key, factor):
-                a1 = lt[key][0]
-                nc.scalar.activation(out=a1[:], in_=a1[:], func=ACT.Ln, bias=eps[:], scale=factor * RHO / WB)
-
-            def zed1(q):
+            for k in range(4):
                 nc.vector.tensor_tensor(
-                    out=z1[:, :, q, :], in0=z1[:, :, q, :],
-                    in1=lt[(1, q)][0][:].rearrange("p (k h) -> p k h", h=CH), op=ALU.subtract,
+                    out=z1[:, k], in0=z1[:, k], in1=ll1[:, :, CH * k : CH * k + CH], op=ALU.subtract
                 )
-
-            def zed2(q):
-                g, t0 = q // 2, 2 * (q % 2)
-                zv = z2[:, 2 * g : 2 * g + 2, t0 : t0 + 2, :]
-                nc.vector.tensor_tensor(
-                    out=zv, in0=zv, in1=lt[(2, q)][0][:].rearrange("p (t k h) -> p k t h", t=2, h=CH),
-                    op=ALU.subtract,
-                )
-
-            def transposes(pair):
-                xt = psx.tile([P, 2, 2, P], F32, name="xt")
-                for rr in range(2):
-                    xw = xsb[:, 2 * pair + rr, :].bitcast(F32)
-                    for u in range(2):
-                        nc.tensor.transpose(xt[:, rr, u, :], xw[:, P * u : P * u + P], ident[:])
-                nc.vector.tensor_copy(
-                    out=xg[:].bitcast(F32)[:, 2 * pair : 2 * pair + 2],
-                    in_=xt[:].rearrange("p r u m -> p r m u"),
-                )
-
-            def quant_x(c):
-                nc.vector.quantize_mx(
-                    out=xc[:, 512 * c : 512 * c + 512].bitcast(FP8X4),
-                    scales=xs[:, 512 * c : 512 * c + 512],
-                    in_=xg[:, 4 * c : 4 * c + 4].rearrange("p r m t -> p (r m t)"),
-                )
-
-            def gate(z, k):
-                nc.scalar.activation(out=z[:, k], in_=z[:, k], func=ACT.Sigmoid)
-
-            def eff(e, z, wview, k):
-                nc.vector.tensor_tensor(
-                    out=e[:, k].rearrange("p (c i) t -> p c t i", i=4),
-                    in0=wview.rearrange("p t (c i) -> p c t i", i=4),
-                    in1=z[:, k].rearrange("p t (c i) -> p c t i", i=4), op=ALU.mult,
-                )
-
-            def quant_w(e, cw, sw, k):
-                nc.vector.quantize_mx(
-                    out=cw[:, CH * k : CH * k + CH].bitcast(FP8X4),
-                    scales=sw[:, CH * k : CH * k + CH],
-                    in_=e[:, k].rearrange("p h t -> p (h t)"),
-                )
-
-            def len2_v(q):
-                if q in ABS2:
-                    abs_v((2, q))
-                else:
-                    max_v((2, q), [2 * q, 2 * q + 1])
-
-            for q in range(4):
-                abs_s((1, q), hxp, hyp, nip, [q])
-            for q in ABS2:
-                abs_s((2, q), oxp, oyp, nhp, [2 * q, 2 * q + 1])
-            len2_v(0)
-            abs_v((1, 0))
-            clamp(wc1, w1sb)
-            abs_v((1, 1))
-            len2_v(1)
-            abs_v((1, 2))
-            abs_v((1, 3))
-            clamp(wc2, w2sb)
-            ln_width(z1, wc1, 0, 4)
-            for q in range(4):
-                ln_len((1, q), 1.0)
-            len2_v(2)
-            zed1(0)
-            zed1(1)
-            len2_v(3)
             ln_width(z2, wc2, 0, 2)
             ln_width(z2, wc2, 1, 2)
             for q in range(4):
-                ln_len((2, q), 1.0 if q in ABS2 else 2.0)
-            zed1(2)
-            zed1(3)
+                nc.scalar.activation(
+                    out=ll2[:, 2 * q : 2 * q + 2, :], in_=ll2[:, 2 * q : 2 * q + 2, :], func=ACT.Ln,
+                    bias=eps[:], scale=2.0 * RHO / WB,
+                )
             transposes(0)
             transposes(1)
             quant_x(0)
             b1f = const.tile([P, 8], F32)
             nc.vector.tensor_copy(out=b1f[:], in_=b1sb[:])
             for q in range(4):
-                zed2(q)
+                g, t0 = q // 2, 2 * (q % 2)
+                zv = z2[:, 2 * g : 2 * g + 2, t0 : t0 + 2, :]
+                nc.vector.tensor_tensor(
+                    out=zv, in0=zv,
+                    in1=ll2[:, 2 * q : 2 * q + 2, :].rearrange("p t (k h) -> p k t h", h=CH),
+                    op=ALU.subtract,
+                )
 
         psa = ctx.enter_context(tc.psum_pool(name="psa", bufs=4))
         psb = ctx.enter_context(tc.psum_pool(name="psb", bufs=2))

@@ -14,12 +14,12 @@ ALU = mybir.AluOpType
 P = 128
 B, I, H, O = 2048, 512, 1024, 512
 FLOPS = 2 * B * I * H + 2 * B * H * O
-RHO = 1.68e-8 / 35e-6
 WA = (5.0 - 0.09) / 6.0
-WB = 0.09 + (5.0 - 0.09) / 2.0
-EPS = 1e-18
+BETA = (0.09 + (5.0 - 0.09) / 2.0) / WA
+RW = 1.68e-8 / 35e-6 / WA
 CH = 256
-SCALAR_PAIRS = (7,)
+KAP = 16.0
+SCALAR_PAIRS = ()
 
 
 def tile_physicalneuralnetwork_kernel(
@@ -29,10 +29,8 @@ def tile_physicalneuralnetwork_kernel(
     with ExitStack() as ctx:
         const = ctx.enter_context(tc.tile_pool(name="const", bufs=1))
         w8 = ctx.enter_context(tc.tile_pool(name="w8", bufs=2))
-        atp = ctx.enter_context(tc.tile_pool(name="atp", bufs=3))
         hp = ctx.enter_context(tc.tile_pool(name="hp", bufs=2))
         hq = ctx.enter_context(tc.tile_pool(name="hq", bufs=3))
-        op = ctx.enter_context(tc.tile_pool(name="op", bufs=6))
         psx = ctx.enter_context(tc.psum_pool(name="psx", bufs=2))
         ctx.enter_context(nc.allow_non_contiguous_dma(reason="small per-partition vectors"))
 
@@ -50,30 +48,37 @@ def tile_physicalneuralnetwork_kernel(
             out=w1sb[:].rearrange("p (u e) h -> p u (e h)", u=2),
             in_=W1.rearrange("(u p e) h -> p u (e h)", u=2, e=2),
         )
-        xsb = const.tile([P, 16, I], BF16)
-        xv = x.rearrange("(m r) i -> m r i", r=16)
-        nc.sync.dma_start(out=xsb[:, 0:4, :], in_=xv[:, 0:4, :])
+        rowh = const.tile([P, H], BF16)
+        nc.vector.memset(rowh[:], 0.0)
+        nc.sync.dma_start(out=rowh[0:1, :], in_=hidden_positions[512:1024, :].rearrange("(a h) c -> a (h c)", a=1))
+        opos = const.tile([P, 4, 2], BF16)
+        nc.sync.dma_start(out=opos[:], in_=output_positions.rearrange("(a p) c -> p a c", p=P))
         w2sb = const.tile([P, 8, O], BF16)
         nc.sync.dma_start(out=w2sb[:], in_=W2.rearrange("(a p) o -> p a o", p=P))
-        for c in range(1, 4):
+        xsb = const.tile([P, 16, I], BF16)
+        xv = x.rearrange("(m r) i -> m r i", r=16)
+        for c in range(4):
             nc.sync.dma_start(out=xsb[:, 4 * c : 4 * c + 4, :], in_=xv[:, 4 * c : 4 * c + 4, :])
         b1sb = const.tile([P, 8], BF16)
         nc.sync.dma_start(out=b1sb[:], in_=b1.rearrange("(a p) -> p a", p=P))
 
         ident = const.tile([P, P], F32)
         make_identity(nc, ident[:])
+        identb = const.tile([P, P], BF16)
+        make_identity(nc, identb[:])
 
         xg = const.tile([P, 16, P, 4], BF16, align_bytes=64)
         xc = const.tile([P, B], U32, align_bytes=64)
         xs = const.tile([P, B], U8, align_bytes=64)
-        z1 = const.tile([P, 4, 4, CH], F32)
-        z2 = const.tile([P, 4, 4, CH], F32)
+        u1 = const.tile([P, 4, H], F32)
+        u2 = const.tile([P, 8, O], F32)
         ll1 = const.tile([P, 4, H], F32)
         ll2 = const.tile([P, 8, O], F32)
         c1 = const.tile([P, 4 * CH], U32, align_bytes=64)
         s1 = const.tile([P, 4 * CH], U8, align_bytes=64)
         c2 = const.tile([P, 4 * CH], U32, align_bytes=64)
         s2 = const.tile([P, 4 * CH], U8, align_bytes=64)
+        zero = const.tile([P, 1], F32)
         wc1 = w8.tile([P, 4, H], BF16, name="wc1", tag="w8", align_bytes=64)
         wc2 = w8.tile([P, 8, O], BF16, name="wc2", tag="w8", align_bytes=64)
 
@@ -81,13 +86,18 @@ def tile_physicalneuralnetwork_kernel(
             nc.vector.tensor_scalar(
                 out=wc[:], in0=wsb[:], scalar1=-3.0, scalar2=3.0, op0=ALU.max, op1=ALU.min
             )
+            nc.vector.tensor_scalar_mul(out=wsb[:], in0=wsb[:], scalar1=KAP)
 
-        def ln_width(z, wc, g, kper):
-            nc.scalar.activation(
-                out=z[:, g * kper : (g + 1) * kper],
-                in_=wc[:, 4 * g : 4 * g + 4, :].rearrange("p t (k h) -> p k t h", h=CH),
-                func=ACT.Ln, bias=one[:], scale=WA / WB,
-            )
+        def numer(u, wc, wsb, q, on_gpsimd):
+            cols = slice(1024 * q, 1024 * q + 1024)
+            uv = u[:].rearrange("p j n -> p (j n)")[:, cols]
+            cv = wc[:].rearrange("p j n -> p (j n)")[:, cols]
+            wv = wsb[:].rearrange("p j n -> p (j n)")[:, cols]
+            if on_gpsimd:
+                nc.gpsimd.tensor_scalar(out=uv, in0=cv, scalar1=1.0, scalar2=BETA, op0=ALU.mult, op1=ALU.add)
+                nc.gpsimd.tensor_tensor(out=uv, in0=uv, in1=wv, op=ALU.mult)
+            else:
+                nc.vector.scalar_tensor_tensor(out=uv, in0=cv, scalar=BETA, in1=wv, op0=ALU.add, op1=ALU.mult)
 
         def transposes(pair):
             xt = psx.tile([P, 2, 2, P], F32, name="xt")
@@ -109,14 +119,14 @@ def tile_physicalneuralnetwork_kernel(
                 in_=xg[:, 4 * c : 4 * c + 4].rearrange("p r m t -> p (r m t)"),
             )
 
-        def gate(z, k):
-            nc.scalar.activation(out=z[:, k], in_=z[:, k], func=ACT.Sigmoid)
+        def recip(lv):
+            nc.scalar.activation(out=lv, in_=lv, func=ACT.Sigmoid, bias=zero[:], scale=-1.0)
 
-        def eff(e, z, wview, k):
+        def eff(e, uv, lv, k):
             nc.vector.tensor_tensor(
                 out=e[:, k].rearrange("p (c i) t -> p c t i", i=4),
-                in0=wview.rearrange("p t (c i) -> p c t i", i=4),
-                in1=z[:, k].rearrange("p t (c i) -> p c t i", i=4), op=ALU.mult,
+                in0=uv.rearrange("p t (c i) -> p c t i", i=4),
+                in1=lv.rearrange("p t (c i) -> p c t i", i=4), op=ALU.mult,
             )
 
         def quant_w(e, cw, sw, k):
@@ -126,7 +136,9 @@ def tile_physicalneuralnetwork_kernel(
                 in_=e[:, k].rearrange("p h t -> p (h t)"),
             )
 
-        with tc.psum_pool(name="psp", bufs=1) as psp, tc.psum_pool(name="psl", bufs=2) as psl:
+        with tc.psum_pool(name="psp", bufs=1) as psp, tc.psum_pool(name="psl", bufs=2) as psl, tc.tile_pool(
+            name="atp", bufs=3
+        ) as atp:
             ones = const.tile([P, P], BF16)
             nc.vector.memset(ones[:], 1.0)
 
@@ -136,40 +148,40 @@ def tile_physicalneuralnetwork_kernel(
                 return t
 
             iv = rowi[:].rearrange("k (u p e c) -> k c u e p", u=2, p=P, e=2, c=2)
-            ixp = spread(psp, iv[:, 0], "ix", "ix")
-            iyp = spread(psp, iv[:, 1], "iy", "iy")
+            ixp = spread(psp, iv[:, 0], "ix", "fx")
+            iyp = spread(psp, iv[:, 1], "iy", "fy")
             oxp = spread(psp, row2[:, 0:1024:2], "ox", "ox")
             oyp = spread(psp, row2[:, 1:1024:2], "oy", "oy")
             b2p = spread(psx, row2[:, 1024:1536], "b2p", "xt")
 
-            eps = const.tile([P, 1], F32)
-            nc.vector.memset(eps[:], EPS)
             one = const.tile([P, 1], F32)
             nc.vector.memset(one[:], 1.0)
             warm = const.tile([P, 1], F32)
             nc.scalar.activation(out=warm[:], in_=one[:], func=ACT.Ln)
-            nhp = const.tile([P, 16], F32)
-            nc.vector.tensor_scalar_mul(out=nhp[:], in0=hpos[:].rearrange("p a c -> p (a c)"), scalar1=-1.0)
+            shp = const.tile([P, 16], F32)
+            nc.vector.tensor_scalar_mul(out=shp[:], in0=hpos[:].rearrange("p a c -> p (a c)"), scalar1=-RW)
+            beta = const.tile([P, 1], F32)
+            nc.vector.tensor_scalar_mul(out=beta[:], in0=one[:], scalar1=KAP * BETA - 1.0)
             hpf = const.tile([P, 8, 2], F32)
             nc.vector.tensor_copy(out=hpf[:], in_=hpos[:])
-            nhs = const.tile([P, 8], F32)
-            nc.vector.tensor_tensor(out=nhs[:], in0=hpf[:, :, 0], in1=hpf[:, :, 1], op=ALU.add)
-            nc.vector.tensor_scalar_mul(out=nhs[:], in0=nhs[:], scalar1=-0.5)
+            bd = const.tile([P, 8], F32)
+            nc.vector.tensor_tensor(out=bd[:], in0=hpf[:, :, 0], in1=hpf[:, :, 1], op=ALU.add)
+            nc.vector.tensor_scalar(
+                out=bd[:], in0=bd[:], scalar1=-KAP * RW, scalar2=KAP * BETA - 1.0, op0=ALU.mult, op1=ALU.add
+            )
             nos = const.tile([P, O], F32)
             nc.vector.tensor_scalar_mul(out=nos[:], in0=oxp[:], scalar1=-0.5)
             nc.vector.scalar_tensor_tensor(
                 out=nos[:], in0=oyp[:], scalar=-0.5, in1=nos[:], op0=ALU.mult, op1=ALU.add
             )
+            sop = const.tile([P, 8], F32)
+            nc.vector.tensor_scalar_mul(out=sop[:], in0=opos[:].rearrange("p a c -> p (a c)"), scalar1=-RW)
 
-            def len1(hb):
+            def denom_t(fx, fy, bias, col, wcv):
                 atx = atp.tile([P, 512], F32, name="atx")
                 aty = atp.tile([P, 512], F32, name="aty")
-                nc.scalar.activation(
-                    out=atx[:], in_=ixp[:], func=ACT.Abs, bias=nhp[:, 2 * hb : 2 * hb + 1], scale=1.0
-                )
-                nc.scalar.activation(
-                    out=aty[:], in_=iyp[:], func=ACT.Abs, bias=nhp[:, 2 * hb + 1 : 2 * hb + 2], scale=1.0
-                )
+                nc.scalar.activation(out=atx[:], in_=fx[:], func=ACT.Abs, bias=bias[:, col : col + 1], scale=RW)
+                nc.scalar.activation(out=aty[:], in_=fy[:], func=ACT.Abs, bias=bias[:, col + 1 : col + 2], scale=RW)
                 xl = psl.tile([P, 4, P], F32, name="xl")
                 for t in range(4):
                     nc.tensor.matmul(
@@ -178,16 +190,15 @@ def tile_physicalneuralnetwork_kernel(
                     )
                     nc.tensor.matmul(
                         out=xl[:, t, :], lhsT=aty[:, P * t : P * t + P], rhs=ident[:],
-                        is_transpose=True, start=False, stop=True,
+                        is_transpose=True, start=False, stop=False,
                     )
+                    nc.tensor.matmul(out=xl[:, t, :], lhsT=identb[:], rhs=wcv[:, t, :], start=False, stop=True)
                 return xl
 
-            def ln_len1(hb, xl):
-                nc.scalar.activation(
-                    out=ll1[:, :, P * hb : P * hb + P], in_=xl[:], func=ACT.Ln, bias=eps[:], scale=RHO / WB
-                )
+            def ln_t(lv, xl):
+                nc.scalar.activation(out=lv, in_=xl[:], func=ACT.Ln, bias=beta[:], scale=KAP)
 
-            def len2(j):
+            def denom_v(j):
                 sl = ll2[:, j, :]
                 nc.vector.scalar_tensor_tensor(
                     out=sl, in0=oxp[:], scalar=hpf[:, j, 0:1], in1=nos[:], op0=ALU.max, op1=ALU.add
@@ -195,70 +206,73 @@ def tile_physicalneuralnetwork_kernel(
                 nc.vector.scalar_tensor_tensor(
                     out=sl, in0=oyp[:], scalar=hpf[:, j, 1:2], in1=sl, op0=ALU.max, op1=ALU.add
                 )
-                nc.vector.tensor_scalar(
-                    out=sl, in0=sl, scalar1=nhs[:, j : j + 1], scalar2=0.0, op0=ALU.add, op1=ALU.max
+                nc.vector.scalar_tensor_tensor(
+                    out=sl, in0=sl, scalar=2.0 * RW, in1=wc2[:, j, :], op0=ALU.mult, op1=ALU.add
                 )
 
-            xls = {}
-            xls[0] = len1(0)
-            len2(0)
-            len2(1)
             clamp(wc1, w1sb)
-            for hb in range(1, 8):
-                xls[hb] = len1(hb)
-                ln_len1(hb - 1, xls[hb - 1])
-                if hb < 7:
-                    len2(hb + 1)
-            ln_len1(7, xls[7])
-            ln_width(z1, wc1, 0, 4)
+            for q in range(4):
+                numer(u1, wc1, w1sb, q, True)
             clamp(wc2, w2sb)
+            xls = {}
+            for hb in range(8):
+                xls[hb] = denom_t(ixp, iyp, shp, 2 * hb, wc1[:, :, P * hb : P * hb + P])
+                if hb > 0:
+                    ln_t(ll1[:, :, P * (hb - 1) : P * hb], xls[hb - 1])
+                if hb < 4:
+                    denom_v(hb)
+            hxp = spread(psp, rowh[:, 0:1024:2], "hx", "fx")
+            hyp = spread(psp, rowh[:, 1:1024:2], "hy", "fy")
+            for ob in range(4):
+                xls[8 + ob] = denom_t(hxp, hyp, sop, 2 * ob, wc2[:, 4:8, P * ob : P * ob + P])
+                if ob == 0:
+                    ln_t(ll1[:, :, P * 7 : P * 8], xls[7])
+                else:
+                    ln_t(ll2[:, 4:8, P * (ob - 1) : P * ob], xls[7 + ob])
+            ln_t(ll2[:, 4:8, P * 3 : P * 4], xls[11])
+            for j in range(4):
+                nc.scalar.activation(
+                    out=ll2[:, j, :], in_=ll2[:, j, :], func=ACT.Ln, bias=bd[:, j : j + 1], scale=KAP
+                )
+            nc.vector.tensor_scalar_mul(out=zero[:], in0=ll2[:, 7, O - 1 : O], scalar1=0.0)
+            nc.vector.scalar_tensor_tensor(
+                out=zero[:], in0=ll2[:, 3, O - 1 : O], scalar=0.0, in1=zero[:], op0=ALU.mult, op1=ALU.add
+            )
             b2b = const.tile([P, O], F32)
             nc.vector.tensor_copy(out=b2b[:], in_=b2p[:])
-            for k in range(4):
-                nc.vector.tensor_tensor(
-                    out=z1[:, k], in0=z1[:, k], in1=ll1[:, :, CH * k : CH * k + CH], op=ALU.subtract
-                )
-            ln_width(z2, wc2, 0, 2)
-            ln_width(z2, wc2, 1, 2)
-            for q in range(4):
-                nc.scalar.activation(
-                    out=ll2[:, 2 * q : 2 * q + 2, :], in_=ll2[:, 2 * q : 2 * q + 2, :], func=ACT.Ln,
-                    bias=eps[:], scale=2.0 * RHO / WB,
-                )
             transposes(0)
             transposes(1)
             quant_x(0)
             b1f = const.tile([P, 8], F32)
             nc.vector.tensor_copy(out=b1f[:], in_=b1sb[:])
             for q in range(4):
-                g, t0 = q // 2, 2 * (q % 2)
-                zv = z2[:, 2 * g : 2 * g + 2, t0 : t0 + 2, :]
-                nc.vector.tensor_tensor(
-                    out=zv, in0=zv,
-                    in1=ll2[:, 2 * q : 2 * q + 2, :].rearrange("p t (k h) -> p k t h", h=CH),
-                    op=ALU.subtract,
-                )
+                numer(u2, wc2, w2sb, q, False)
 
         psa = ctx.enter_context(tc.psum_pool(name="psa", bufs=4))
         psb = ctx.enter_context(tc.psum_pool(name="psb", bufs=2))
+        op = ctx.enter_context(tc.tile_pool(name="op", bufs=10))
 
         e1 = w8.tile([P, 4, CH, 4], BF16, name="e1", tag="w8", align_bytes=64)
         e2 = w8.tile([P, 4, CH, 4], BF16, name="e2", tag="w8", align_bytes=64)
+
+        def view2(t, k):
+            g, oh = k // 2, k % 2
+            return t[:, 4 * g : 4 * g + 4, CH * oh : CH * oh + CH]
+
         for k in range(4):
-            gate(z1, k)
-            eff(e1, z1, w1sb[:, :, CH * k : CH * k + CH], k)
+            recip(ll1[:, :, CH * k : CH * k + CH])
+            eff(e1, u1[:, :, CH * k : CH * k + CH], ll1[:, :, CH * k : CH * k + CH], k)
             if k > 0:
                 quant_w(e1, c1, s1, k - 1)
         for k in range(4):
-            gate(z2, k)
+            recip(view2(ll2, k))
         transposes(2)
         quant_w(e1, c1, s1, 3)
         transposes(3)
         quant_x(1)
 
         def eff2(k):
-            g, oh = k // 2, k % 2
-            eff(e2, z2, w2sb[:, 4 * g : 4 * g + 4, CH * oh : CH * oh + CH], k)
+            eff(e2, view2(u2, k), view2(ll2, k), k)
 
         ov = out.rearrange("(m r) o -> m r o", r=16)
         hid = {}

@@ -19,7 +19,7 @@ BETA = (0.09 + (5.0 - 0.09) / 2.0) / WA
 RW = 1.68e-8 / 35e-6 / WA
 CH = 256
 KAP = 16.0
-SCALAR_PAIRS = ()
+SCALAR_PAIRS = (4, 5, 6, 7)
 
 
 def tile_physicalneuralnetwork_kernel(
@@ -186,13 +186,13 @@ def tile_physicalneuralnetwork_kernel(
                 for t in range(4):
                     nc.tensor.matmul(
                         out=xl[:, t, :], lhsT=atx[:, P * t : P * t + P], rhs=ident[:],
-                        is_transpose=True, start=True, stop=False,
+                        is_transpose=True, start=(t == 0), stop=False,
                     )
                     nc.tensor.matmul(
                         out=xl[:, t, :], lhsT=aty[:, P * t : P * t + P], rhs=ident[:],
                         is_transpose=True, start=False, stop=False,
                     )
-                    nc.tensor.matmul(out=xl[:, t, :], lhsT=identb[:], rhs=wcv[:, t, :], start=False, stop=True)
+                nc.tensor.matmul(out=xl[:], lhsT=identb[:], rhs=wcv, start=False, stop=True)
                 return xl
 
             def ln_t(lv, xl):
@@ -212,7 +212,7 @@ def tile_physicalneuralnetwork_kernel(
 
             clamp(wc1, w1sb)
             for q in range(4):
-                numer(u1, wc1, w1sb, q, True)
+                numer(u1, wc1, w1sb, q, False)
             clamp(wc2, w2sb)
             xls = {}
             for hb in range(8):

@@ -19,7 +19,6 @@ BETA = (0.09 + (5.0 - 0.09) / 2.0) / WA
 RW = 1.68e-8 / 35e-6 / WA
 CH = 256
 KAP = 16.0
-SCALAR_PAIRS = (4, 5, 6, 7)
 
 
 def tile_physicalneuralnetwork_kernel(
@@ -29,30 +28,38 @@ def tile_physicalneuralnetwork_kernel(
     with ExitStack() as ctx:
         const = ctx.enter_context(tc.tile_pool(name="const", bufs=1))
         w8 = ctx.enter_context(tc.tile_pool(name="w8", bufs=2))
-        hp = ctx.enter_context(tc.tile_pool(name="hp", bufs=2))
-        hq = ctx.enter_context(tc.tile_pool(name="hq", bufs=3))
         psx = ctx.enter_context(tc.psum_pool(name="psx", bufs=2))
+        ctx.enter_context(tc.manual_schedule())
         ctx.enter_context(nc.allow_non_contiguous_dma(reason="small per-partition vectors"))
 
         rowi = const.tile([P, 2 * I], BF16)
-        nc.vector.memset(rowi[:], 0.0)
+        nc.vector.memset(rowi[:].bitcast(U32), 0)
         nc.sync.dma_start(out=rowi[0:1, :], in_=input_positions.rearrange("(a h) c -> a (h c)", a=1))
+        one = const.tile([P, 1], F32)
+        nc.vector.memset(one[:], 1.0)
+        ones = const.tile([P, P], BF16)
+        nc.vector.memset(ones[:], 1.0)
         hpos = const.tile([P, 8, 2], BF16)
         nc.sync.dma_start(out=hpos[:], in_=hidden_positions.rearrange("(a p) c -> p a c", p=P))
-        row2 = const.tile([P, 3 * O], BF16)
-        nc.vector.memset(row2[:], 0.0)
-        nc.sync.dma_start(out=row2[0:1, 0 : 2 * O], in_=output_positions.rearrange("(a h) c -> a (h c)", a=1))
-        nc.sync.dma_start(out=row2[0:1, 2 * O : 3 * O], in_=b2.rearrange("(a o) -> a o", a=1))
-        w1sb = const.tile([P, 4, H], BF16)
-        nc.sync.dma_start(
-            out=w1sb[:].rearrange("p (u e) h -> p u (e h)", u=2),
-            in_=W1.rearrange("(u p e) h -> p u (e h)", u=2, e=2),
-        )
-        rowh = const.tile([P, H], BF16)
-        nc.vector.memset(rowh[:], 0.0)
-        nc.sync.dma_start(out=rowh[0:1, :], in_=hidden_positions[512:1024, :].rearrange("(a h) c -> a (h c)", a=1))
+        rowh = const.tile([P, 2 * H], BF16)
+        nc.gpsimd.memset(rowh[:].bitcast(U32), 0)
+        nc.sync.dma_start(out=rowh[0:1, :], in_=hidden_positions.rearrange("(a h) c -> a (h c)", a=1))
         opos = const.tile([P, 4, 2], BF16)
         nc.sync.dma_start(out=opos[:], in_=output_positions.rearrange("(a p) c -> p a c", p=P))
+        ipos = const.tile([P, 4, 2], BF16)
+        nc.sync.dma_start(
+            out=ipos[:].rearrange("p (u e) c -> p u (e c)", u=2),
+            in_=input_positions.rearrange("(u p e) c -> p u (e c)", u=2, e=2),
+        )
+        w1sb = const.tile([P, 4, H], BF16)
+        for u in range(2):
+            nc.sync.dma_start(
+                out=w1sb[:, 2 * u : 2 * u + 2, :].rearrange("p e h -> p (e h)"),
+                in_=W1[256 * u : 256 * u + 256, :].rearrange("(p e) h -> p (e h)", e=2),
+            )
+        rowb = const.tile([P, O], BF16)
+        nc.gpsimd.memset(rowb[:].bitcast(U32), 0)
+        nc.sync.dma_start(out=rowb[0:1, :], in_=b2.rearrange("(a o) -> a o", a=1))
         w2sb = const.tile([P, 8, O], BF16)
         nc.sync.dma_start(out=w2sb[:], in_=W2.rearrange("(a p) o -> p a o", p=P))
         xsb = const.tile([P, 16, I], BF16)
@@ -78,26 +85,25 @@ def tile_physicalneuralnetwork_kernel(
         s1 = const.tile([P, 4 * CH], U8, align_bytes=64)
         c2 = const.tile([P, 4 * CH], U32, align_bytes=64)
         s2 = const.tile([P, 4 * CH], U8, align_bytes=64)
-        zero = const.tile([P, 1], F32)
         wc1 = w8.tile([P, 4, H], BF16, name="wc1", tag="w8", align_bytes=64)
         wc2 = w8.tile([P, 8, O], BF16, name="wc2", tag="w8", align_bytes=64)
 
-        def clamp(wc, wsb):
+        def clamp(layer, u):
+            wc, wsb = (wc1, w1sb) if layer == 1 else (wc2, w2sb)
+            n = wc.shape[1] // 2
             nc.vector.tensor_scalar(
-                out=wc[:], in0=wsb[:], scalar1=-3.0, scalar2=3.0, op0=ALU.max, op1=ALU.min
+                out=wc[:, n * u : n * u + n], in0=wsb[:, n * u : n * u + n], scalar1=-3.0, scalar2=3.0,
+                op0=ALU.max, op1=ALU.min,
             )
-            nc.vector.tensor_scalar_mul(out=wsb[:], in0=wsb[:], scalar1=KAP)
 
-        def numer(u, wc, wsb, q, on_gpsimd):
+        def numer(u, wc, wsb, q):
             cols = slice(1024 * q, 1024 * q + 1024)
             uv = u[:].rearrange("p j n -> p (j n)")[:, cols]
             cv = wc[:].rearrange("p j n -> p (j n)")[:, cols]
             wv = wsb[:].rearrange("p j n -> p (j n)")[:, cols]
-            if on_gpsimd:
-                nc.gpsimd.tensor_scalar(out=uv, in0=cv, scalar1=1.0, scalar2=BETA, op0=ALU.mult, op1=ALU.add)
-                nc.gpsimd.tensor_tensor(out=uv, in0=uv, in1=wv, op=ALU.mult)
-            else:
-                nc.vector.scalar_tensor_tensor(out=uv, in0=cv, scalar=BETA, in1=wv, op0=ALU.add, op1=ALU.mult)
+            nc.vector.scalar_tensor_tensor(out=uv, in0=cv, scalar=BETA, in1=wv, op0=ALU.add, op1=ALU.mult)
+
+        xts = {}
 
         def transposes(pair):
             xt = psx.tile([P, 2, 2, P], F32, name="xt")
@@ -105,9 +111,12 @@ def tile_physicalneuralnetwork_kernel(
                 xw = xsb[:, 2 * pair + rr, :].bitcast(F32)
                 for u in range(2):
                     nc.tensor.transpose(xt[:, rr, u, :], xw[:, P * u : P * u + P], ident[:])
+            xts[pair] = xt
+
+        def copy_x(pair, on_scalar):
             dst = xg[:].bitcast(F32)[:, 2 * pair : 2 * pair + 2]
-            src = xt[:].rearrange("p r u m -> p r m u")
-            if pair in SCALAR_PAIRS:
+            src = xts[pair][:].rearrange("p r u m -> p r m u")
+            if on_scalar:
                 nc.scalar.copy(out=dst, in_=src)
             else:
                 nc.vector.tensor_copy(out=dst, in_=src)
@@ -120,7 +129,7 @@ def tile_physicalneuralnetwork_kernel(
             )
 
         def recip(lv):
-            nc.scalar.activation(out=lv, in_=lv, func=ACT.Sigmoid, bias=zero[:], scale=-1.0)
+            nc.scalar.activation(out=lv, in_=lv, func=ACT.Sigmoid, scale=-1.0)
 
         def eff(e, uv, lv, k):
             nc.vector.tensor_tensor(
@@ -136,120 +145,137 @@ def tile_physicalneuralnetwork_kernel(
                 in_=e[:, k].rearrange("p h t -> p (h t)"),
             )
 
-        with tc.psum_pool(name="psp", bufs=1) as psp, tc.psum_pool(name="psl", bufs=2) as psl, tc.tile_pool(
-            name="atp", bufs=3
-        ) as atp:
-            ones = const.tile([P, P], BF16)
-            nc.vector.memset(ones[:], 1.0)
-
+        with tc.psum_pool(name="psp", bufs=1) as psp, tc.psum_pool(name="psl", bufs=4) as psl, tc.tile_pool(
+            name="pl", bufs=8
+        ) as pl:
             def spread(pool, src, name, tag):
                 t = pool.tile([P, 512], F32, name=name, tag=tag)
                 nc.tensor.matmul(out=t[:], lhsT=ones[:], rhs=src, start=True, stop=True)
                 return t
 
             iv = rowi[:].rearrange("k (u p e c) -> k c u e p", u=2, p=P, e=2, c=2)
-            ixp = spread(psp, iv[:, 0], "ix", "fx")
-            iyp = spread(psp, iv[:, 1], "iy", "fy")
-            oxp = spread(psp, row2[:, 0:1024:2], "ox", "ox")
-            oyp = spread(psp, row2[:, 1:1024:2], "oy", "oy")
-            b2p = spread(psx, row2[:, 1024:1536], "b2p", "xt")
-
-            one = const.tile([P, 1], F32)
-            nc.vector.memset(one[:], 1.0)
             warm = const.tile([P, 1], F32)
             nc.scalar.activation(out=warm[:], in_=one[:], func=ACT.Ln)
-            shp = const.tile([P, 16], F32)
-            nc.vector.tensor_scalar_mul(out=shp[:], in0=hpos[:].rearrange("p a c -> p (a c)"), scalar1=-RW)
-            beta = const.tile([P, 1], F32)
-            nc.vector.tensor_scalar_mul(out=beta[:], in0=one[:], scalar1=KAP * BETA - 1.0)
-            hpf = const.tile([P, 8, 2], F32)
-            nc.vector.tensor_copy(out=hpf[:], in_=hpos[:])
-            bd = const.tile([P, 8], F32)
-            nc.vector.tensor_tensor(out=bd[:], in0=hpf[:, :, 0], in1=hpf[:, :, 1], op=ALU.add)
-            nc.vector.tensor_scalar(
-                out=bd[:], in0=bd[:], scalar1=-KAP * RW, scalar2=KAP * BETA - 1.0, op0=ALU.mult, op1=ALU.add
-            )
-            nos = const.tile([P, O], F32)
-            nc.vector.tensor_scalar_mul(out=nos[:], in0=oxp[:], scalar1=-0.5)
-            nc.vector.scalar_tensor_tensor(
-                out=nos[:], in0=oyp[:], scalar=-0.5, in1=nos[:], op0=ALU.mult, op1=ALU.add
-            )
+            ixy = []
+            ips = [spread(psx, iv[:, c], "ip", "xt") for c in range(2)]
+            fps = {0: [spread(psp, rowh[:, c : 1024 : 2], "fp", "f" + "xy"[c]) for c in range(2)]}
+            for c in range(2):
+                it = const.tile([P, 512], F32, name="i" + "xy"[c])
+                nc.scalar.activation(out=it[:], in_=ips[c][:], func=ACT.Copy, scale=2.0 * RW)
+                ixy.append(it)
+
+            hp2 = const.tile([P, 16], F32)
+            nc.vector.tensor_scalar_mul(out=hp2[:], in0=hpos[:].rearrange("p a c -> p (a c)"), scalar1=2.0 * RW)
+            hp1 = const.tile([P, 16], F32)
+            nc.vector.tensor_scalar_mul(out=hp1[:], in0=hpos[:].rearrange("p a c -> p (a c)"), scalar1=RW)
             sop = const.tile([P, 8], F32)
             nc.vector.tensor_scalar_mul(out=sop[:], in0=opos[:].rearrange("p a c -> p (a c)"), scalar1=-RW)
-
-            def denom_t(fx, fy, bias, col, wcv):
-                atx = atp.tile([P, 512], F32, name="atx")
-                aty = atp.tile([P, 512], F32, name="aty")
-                nc.scalar.activation(out=atx[:], in_=fx[:], func=ACT.Abs, bias=bias[:, col : col + 1], scale=RW)
-                nc.scalar.activation(out=aty[:], in_=fy[:], func=ACT.Abs, bias=bias[:, col + 1 : col + 2], scale=RW)
-                xl = psl.tile([P, 4, P], F32, name="xl")
-                for t in range(4):
-                    nc.tensor.matmul(
-                        out=xl[:, t, :], lhsT=atx[:, P * t : P * t + P], rhs=ident[:],
-                        is_transpose=True, start=(t == 0), stop=False,
-                    )
-                    nc.tensor.matmul(
-                        out=xl[:, t, :], lhsT=aty[:, P * t : P * t + P], rhs=ident[:],
-                        is_transpose=True, start=False, stop=False,
-                    )
-                nc.tensor.matmul(out=xl[:], lhsT=identb[:], rhs=wcv, start=False, stop=True)
-                return xl
-
-            def ln_t(lv, xl):
-                nc.scalar.activation(out=lv, in_=xl[:], func=ACT.Ln, bias=beta[:], scale=KAP)
-
-            def denom_v(j):
-                sl = ll2[:, j, :]
-                nc.vector.scalar_tensor_tensor(
-                    out=sl, in0=oxp[:], scalar=hpf[:, j, 0:1], in1=nos[:], op0=ALU.max, op1=ALU.add
-                )
-                nc.vector.scalar_tensor_tensor(
-                    out=sl, in0=oyp[:], scalar=hpf[:, j, 1:2], in1=sl, op0=ALU.max, op1=ALU.add
-                )
-                nc.vector.scalar_tensor_tensor(
-                    out=sl, in0=sl, scalar=2.0 * RW, in1=wc2[:, j, :], op0=ALU.mult, op1=ALU.add
-                )
-
-            clamp(wc1, w1sb)
-            for q in range(4):
-                numer(u1, wc1, w1sb, q, False)
-            clamp(wc2, w2sb)
-            xls = {}
-            for hb in range(8):
-                xls[hb] = denom_t(ixp, iyp, shp, 2 * hb, wc1[:, :, P * hb : P * hb + P])
-                if hb > 0:
-                    ln_t(ll1[:, :, P * (hb - 1) : P * hb], xls[hb - 1])
-                if hb < 4:
-                    denom_v(hb)
-            hxp = spread(psp, rowh[:, 0:1024:2], "hx", "fx")
-            hyp = spread(psp, rowh[:, 1:1024:2], "hy", "fy")
-            for ob in range(4):
-                xls[8 + ob] = denom_t(hxp, hyp, sop, 2 * ob, wc2[:, 4:8, P * ob : P * ob + P])
-                if ob == 0:
-                    ln_t(ll1[:, :, P * 7 : P * 8], xls[7])
-                else:
-                    ln_t(ll2[:, 4:8, P * (ob - 1) : P * ob], xls[7 + ob])
-            ln_t(ll2[:, 4:8, P * 3 : P * 4], xls[11])
-            for j in range(4):
-                nc.scalar.activation(
-                    out=ll2[:, j, :], in_=ll2[:, j, :], func=ACT.Ln, bias=bd[:, j : j + 1], scale=KAP
-                )
-            nc.vector.tensor_scalar_mul(out=zero[:], in0=ll2[:, 7, O - 1 : O], scalar1=0.0)
-            nc.vector.scalar_tensor_tensor(
-                out=zero[:], in0=ll2[:, 3, O - 1 : O], scalar=0.0, in1=zero[:], op0=ALU.mult, op1=ALU.add
+            beta = const.tile([P, 1], F32)
+            nc.vector.tensor_scalar_mul(out=beta[:], in0=one[:], scalar1=KAP * BETA - 1.0)
+            ipf = const.tile([P, 4, 2], F32)
+            nc.vector.tensor_copy(out=ipf[:], in_=ipos[:])
+            bi = const.tile([P, 4], F32)
+            nc.vector.tensor_tensor(out=bi[:], in0=ipf[:, :, 0], in1=ipf[:, :, 1], op=ALU.add)
+            nc.vector.tensor_scalar(
+                out=bi[:], in0=bi[:], scalar1=-KAP * RW, scalar2=KAP * BETA - 1.0, op0=ALU.mult, op1=ALU.add
             )
+
+            parts = {}
+
+            def part_v(hh, g, c):
+                col = 2 * (4 * hh + g) + c
+                t = pl.tile([P, 512], F32, name="pv", bufs=16)
+                nc.vector.tensor_scalar(
+                    out=t[:], in0=ixy[c][:], scalar1=hp2[:, col : col + 1], scalar2=hp1[:, col : col + 1],
+                    op0=ALU.max, op1=ALU.subtract,
+                )
+                parts[1, hh, g, c] = t
+
+            def part_s(hh, g, c):
+                t = pl.tile([P, 512], F32, name="ps", bufs=16)
+                nc.scalar.activation(
+                    out=t[:], in_=fps[hh][c][:], func=ACT.Abs, bias=sop[:, 2 * g + c : 2 * g + c + 1], scale=RW
+                )
+                parts[2, hh, g, c] = t
+
+            sums = {}
+
+            def total(layer, hh, t):
+                xl = psl.tile([P, 4, P], F32, name="xl")
+                wcv = wc1[:, t, 512 * hh : 512 * hh + 512] if layer == 1 else wc2[:, 4 * hh + t, :]
+                nc.tensor.matmul(out=xl[:], lhsT=identb[:], rhs=wcv, start=True, stop=False)
+                for g in range(4):
+                    for c in range(2):
+                        nc.tensor.matmul(
+                            out=xl[:, g, :], lhsT=parts[layer, hh, g, c][:, P * t : P * t + P], rhs=ident[:],
+                            is_transpose=True, start=False, stop=(g == 3 and c == 1),
+                        )
+                sums[layer, hh, t] = xl
+
+            def log(layer, hh, t):
+                if layer == 1:
+                    lv, bias = ll1[:, t, 512 * hh : 512 * hh + 512], bi[:, t : t + 1]
+                else:
+                    lv, bias = ll2[:, 4 * hh + t, :], beta[:]
+                nc.scalar.activation(out=lv, in_=sums[layer, hh, t][:], func=ACT.Ln, bias=bias, scale=KAP)
+
             b2b = const.tile([P, O], F32)
+            for g in range(4):
+                part_s(0, g, 0)
+            clamp(1, 0)
+            for g in range(4):
+                for c in range(2):
+                    part_v(0, g, c)
+            clamp(1, 1)
+            total(1, 0, 0)
+            fps[1] = [spread(psp, rowh[:, 1024:2048:2], "fp", "fx")]
+            b2p = spread(psx, rowb[:], "b2p", "xt")
+            for g in range(4):
+                part_s(0, g, 1)
+            for t in range(1, 4):
+                total(1, 0, t)
+            fps[1].append(spread(psp, rowh[:, 1025:2048:2], "fp", "fy"))
+            for g in range(4):
+                for c in range(2):
+                    part_v(1, g, c)
+            clamp(2, 0)
+            clamp(2, 1)
+            for t in range(4):
+                log(1, 0, t)
+                part_s(1, t, 0)
+                total(2, 0, t)
+            for q in range(4):
+                numer(u1, wc1, w1sb, q)
             nc.vector.tensor_copy(out=b2b[:], in_=b2p[:])
             transposes(0)
+            for t in range(4):
+                log(2, 0, t)
+                part_s(1, t, 1)
+                total(1, 1, t)
             transposes(1)
-            quant_x(0)
             b1f = const.tile([P, 8], F32)
             nc.vector.tensor_copy(out=b1f[:], in_=b1sb[:])
-            for q in range(4):
-                numer(u2, wc2, w2sb, q, False)
+            copy_x(0, False)
+            numer(u2, wc2, w2sb, 0)
+            copy_x(1, False)
+            numer(u2, wc2, w2sb, 1)
+            quant_x(0)
+            numer(u2, wc2, w2sb, 2)
+            numer(u2, wc2, w2sb, 3)
+            for t in range(4):
+                log(1, 1, t)
+                total(2, 1, t)
+            for t in range(4):
+                log(2, 1, t)
+            for pair in (2, 3):
+                transposes(pair)
+                copy_x(pair, False)
+            quant_x(1)
 
         psa = ctx.enter_context(tc.psum_pool(name="psa", bufs=4))
         psb = ctx.enter_context(tc.psum_pool(name="psb", bufs=2))
+        hp = ctx.enter_context(tc.tile_pool(name="hp", bufs=2))
+        hq = ctx.enter_context(tc.tile_pool(name="hq", bufs=3))
         op = ctx.enter_context(tc.tile_pool(name="op", bufs=10))
 
         e1 = w8.tile([P, 4, CH, 4], BF16, name="e1", tag="w8", align_bytes=64)
@@ -259,17 +285,9 @@ def tile_physicalneuralnetwork_kernel(
             g, oh = k // 2, k % 2
             return t[:, 4 * g : 4 * g + 4, CH * oh : CH * oh + CH]
 
-        for k in range(4):
-            recip(ll1[:, :, CH * k : CH * k + CH])
-            eff(e1, u1[:, :, CH * k : CH * k + CH], ll1[:, :, CH * k : CH * k + CH], k)
-            if k > 0:
-                quant_w(e1, c1, s1, k - 1)
-        for k in range(4):
-            recip(view2(ll2, k))
-        transposes(2)
-        quant_w(e1, c1, s1, 3)
-        transposes(3)
-        quant_x(1)
+        def eff1(k):
+            cols = slice(CH * k, CH * k + CH)
+            eff(e1, u1[:, :, cols], ll1[:, :, cols], k)
 
         def eff2(k):
             eff(e2, view2(u2, k), view2(ll2, k), k)
@@ -296,7 +314,7 @@ def tile_physicalneuralnetwork_kernel(
                     start=True, stop=True,
                 )
                 nc.scalar.activation(
-                    out=hc[:, mt, :], in_=ps[:], func=ACT.Sigmoid, bias=b1f[:, mt : mt + 1], scale=1.0
+                    out=hc[:, mt, :], in_=ps[:], func=ACT.Sigmoid, bias=b1f[:, mt : mt + 1], scale=KAP
                 )
 
         def regroup(c, g):
@@ -328,60 +346,73 @@ def tile_physicalneuralnetwork_kernel(
                 )
             ot = op.tile([P, 512], F32, name="ot")
             outs[(c, rr)] = ot
-            nc.vector.tensor_tensor(out=ot[:], in0=ps2[:], in1=b2b[:], op=ALU.add)
+            nc.vector.scalar_tensor_tensor(
+                out=ot[:], in0=ps2[:], scalar=KAP, in1=b2b[:], op0=ALU.mult, op1=ALU.add
+            )
 
         def l2_out(c, rr):
             ot = outs[(c, rr)]
             nc.scalar.activation(out=ot[:], in_=ot[:], func=ACT.Sigmoid)
             nc.sync.dma_start(out=ov[:, 4 * c + rr, :], in_=ot[:])
 
-        l1_mm(0, range(0, 8))
+        for k in range(4):
+            recip(ll1[:, :, CH * k : CH * k + CH])
+        for k in range(4):
+            recip(view2(ll2, k))
+        for k in range(4):
+            eff1(k)
+            if k > 0:
+                quant_w(e1, c1, s1, k - 1)
         eff2(0)
-        eff2(1)
-        quant_w(e2, c2, s2, 0)
+        quant_w(e1, c1, s1, 3)
+        for k in range(1, 4):
+            eff2(k)
+            quant_w(e2, c2, s2, k - 1)
+        l1_mm(0, range(0, 8))
+        for pair in (4, 5):
+            transposes(pair)
+            copy_x(pair, True)
         regroup(0, 0)
-        quant_w(e2, c2, s2, 1)
-        transposes(4)
-        quant_h(0, 0)
-        transposes(5)
-        regroup(0, 1)
-        quant_x(2)
-        l1_mm(1, range(0, 8))
-        eff2(2)
-        quant_h(0, 1)
-        eff2(3)
-        quant_w(e2, c2, s2, 2)
-        regroup(1, 0)
         quant_w(e2, c2, s2, 3)
-        transposes(6)
-        quant_h(1, 0)
-        transposes(7)
+        regroup(0, 1)
+        quant_h(0, 0)
+        quant_x(2)
+        quant_h(0, 1)
+        l1_mm(1, range(0, 8))
+        for pair in (6, 7):
+            transposes(pair)
+            copy_x(pair, True)
+        l1_mm(2, range(0, 2))
+        regroup(1, 0)
+        l2_mm(0, 0)
+        l2_mm(0, 1)
         regroup(1, 1)
+        quant_h(1, 0)
         quant_x(3)
-        l1_mm(2, range(0, 8))
-        for rr in range(4):
-            l2_mm(0, rr)
+        l2_mm(0, 2)
+        l2_mm(0, 3)
         quant_h(1, 1)
-        regroup(2, 0)
+        l1_mm(2, range(2, 8))
         for rr in range(4):
             l2_out(0, rr)
-        l1_mm(3, range(0, 8))
+        regroup(2, 0)
         l2_mm(1, 0)
-        quant_h(2, 0)
-        regroup(2, 1)
         l2_mm(1, 1)
-        quant_h(2, 1)
+        regroup(2, 1)
         l2_mm(1, 2)
         l2_mm(1, 3)
-        regroup(3, 0)
+        l1_mm(3, range(0, 8))
+        quant_h(2, 0)
+        quant_h(2, 1)
         for rr in range(4):
             l2_out(1, rr)
+        regroup(3, 0)
         l2_mm(2, 0)
-        quant_h(3, 0)
         l2_mm(2, 1)
         regroup(3, 1)
-        l2_mm(2, 2)
+        quant_h(3, 0)
         quant_h(3, 1)
+        l2_mm(2, 2)
         l2_mm(2, 3)
         for rr in range(4):
             l2_out(2, rr)

@@ -32,47 +32,39 @@ def tile_physicalneuralnetwork_kernel(
         ctx.enter_context(tc.manual_schedule())
         ctx.enter_context(nc.allow_non_contiguous_dma(reason="small per-partition vectors"))
 
-        rowi = const.tile([P, 2 * I], BF16)
-        nc.vector.memset(rowi[:].bitcast(U32), 0)
-        nc.sync.dma_start(out=rowi[0:1, :], in_=input_positions.rearrange("(a h) c -> a (h c)", a=1))
+        rows = const.tile([P, 1024], BF16)
+        nc.vector.memset(rows[:].bitcast(U32)[:, 0:256], 0)
+        nc.gpsimd.memset(rows[:].bitcast(U32)[:, 256:512], 0)
         one = const.tile([P, 1], F32)
         nc.vector.memset(one[:], 1.0)
-        ones = const.tile([P, P], BF16)
-        nc.vector.memset(ones[:], 1.0)
-        hpos = const.tile([P, 8, 2], BF16)
-        nc.sync.dma_start(out=hpos[:], in_=hidden_positions.rearrange("(a p) c -> p a c", p=P))
-        rowh = const.tile([P, 2 * H], BF16)
-        nc.gpsimd.memset(rowh[:].bitcast(U32), 0)
-        nc.sync.dma_start(out=rowh[0:1, :], in_=hidden_positions.rearrange("(a h) c -> a (h c)", a=1))
-        opos = const.tile([P, 4, 2], BF16)
-        nc.sync.dma_start(out=opos[:], in_=output_positions.rearrange("(a p) c -> p a c", p=P))
-        ipos = const.tile([P, 4, 2], BF16)
-        nc.sync.dma_start(
-            out=ipos[:].rearrange("p (u e) c -> p u (e c)", u=2),
-            in_=input_positions.rearrange("(u p e) c -> p u (e c)", u=2, e=2),
-        )
+        cols = const.tile([P, 512], BF16)
+        nc.vector.memset(cols[:].bitcast(U32), 0)
+        nc.sync.dma_start(out=rows[0:1, :], in_=input_positions.rearrange("(a h) c -> a (h c)", a=1))
+        nc.sync.dma_start(out=rows[1:3, :], in_=hidden_positions.rearrange("(a h) c -> a (h c)", a=2))
+        nc.sync.dma_start(out=cols[0:8, 0:256], in_=hidden_positions.rearrange("(a p) c -> a (p c)", p=P))
+        nc.sync.dma_start(out=cols[8:12, 0:256], in_=output_positions.rearrange("(a p) c -> a (p c)", p=P))
+        nc.sync.dma_start(out=cols[12:14, 0:512], in_=input_positions.rearrange("(u r) c -> u (r c)", u=2))
         w1sb = const.tile([P, 4, H], BF16)
         for u in range(2):
             nc.sync.dma_start(
                 out=w1sb[:, 2 * u : 2 * u + 2, :].rearrange("p e h -> p (e h)"),
                 in_=W1[256 * u : 256 * u + 256, :].rearrange("(p e) h -> p (e h)", e=2),
             )
-        rowb = const.tile([P, O], BF16)
-        nc.gpsimd.memset(rowb[:].bitcast(U32), 0)
-        nc.sync.dma_start(out=rowb[0:1, :], in_=b2.rearrange("(a o) -> a o", a=1))
+        biases = const.tile([P, 512], BF16)
+        nc.gpsimd.memset(biases[:].bitcast(U32), 0)
+        nc.sync.dma_start(out=biases[0:8, 0:128], in_=b1.rearrange("(a p) -> a p", p=P))
+        nc.sync.dma_start(out=biases[8:9, :], in_=b2.rearrange("(a o) -> a o", a=1))
         w2sb = const.tile([P, 8, O], BF16)
         nc.sync.dma_start(out=w2sb[:], in_=W2.rearrange("(a p) o -> p a o", p=P))
         xsb = const.tile([P, 16, I], BF16)
         xv = x.rearrange("(m r) i -> m r i", r=16)
         for c in range(4):
             nc.sync.dma_start(out=xsb[:, 4 * c : 4 * c + 4, :], in_=xv[:, 4 * c : 4 * c + 4, :])
-        b1sb = const.tile([P, 8], BF16)
-        nc.sync.dma_start(out=b1sb[:], in_=b1.rearrange("(a p) -> p a", p=P))
 
-        ident = const.tile([P, P], F32)
-        make_identity(nc, ident[:])
         identb = const.tile([P, P], BF16)
         make_identity(nc, identb[:])
+        ident = const.tile([P, P], F32)
+        make_identity(nc, ident[:])
 
         xg = const.tile([P, 16, P, 4], BF16, align_bytes=64)
         xc = const.tile([P, B], U32, align_bytes=64)
@@ -148,34 +140,45 @@ def tile_physicalneuralnetwork_kernel(
         with tc.psum_pool(name="psp", bufs=1) as psp, tc.psum_pool(name="psl", bufs=4) as psl, tc.tile_pool(
             name="pl", bufs=8
         ) as pl:
-            def spread(pool, src, name, tag):
+            def spread(pool, src, row, name, tag):
                 t = pool.tile([P, 512], F32, name=name, tag=tag)
-                nc.tensor.matmul(out=t[:], lhsT=ones[:], rhs=src, start=True, stop=True)
+                nc.tensor.matmul(
+                    out=t[:], lhsT=identb[:, row : row + 1].to_broadcast([P, P]), rhs=src, start=True, stop=True
+                )
                 return t
 
-            iv = rowi[:].rearrange("k (u p e c) -> k c u e p", u=2, p=P, e=2, c=2)
+            def hidden_row(hh, c):
+                return spread(psp, rows[:, c:1024:2], 1 + hh, "fp", "f" + "xy"[c])
+
+            iv = rows[:].rearrange("k (u p e c) -> k c u e p", u=2, p=P, e=2, c=2)
             warm = const.tile([P, 1], F32)
             nc.scalar.activation(out=warm[:], in_=one[:], func=ACT.Ln)
             ixy = []
-            ips = [spread(psx, iv[:, c], "ip", "xt") for c in range(2)]
-            fps = {0: [spread(psp, rowh[:, c : 1024 : 2], "fp", "f" + "xy"[c]) for c in range(2)]}
+            ips = [spread(psx, iv[:, c], 0, "ip", "xt") for c in range(2)]
             for c in range(2):
                 it = const.tile([P, 512], F32, name="i" + "xy"[c])
                 nc.scalar.activation(out=it[:], in_=ips[c][:], func=ACT.Copy, scale=2.0 * RW)
                 ixy.append(it)
 
-            hp2 = const.tile([P, 16], F32)
-            nc.vector.tensor_scalar_mul(out=hp2[:], in0=hpos[:].rearrange("p a c -> p (a c)"), scalar1=2.0 * RW)
-            hp1 = const.tile([P, 16], F32)
-            nc.vector.tensor_scalar_mul(out=hp1[:], in0=hpos[:].rearrange("p a c -> p (a c)"), scalar1=RW)
-            sop = const.tile([P, 8], F32)
-            nc.vector.tensor_scalar_mul(out=sop[:], in0=opos[:].rearrange("p a c -> p (a c)"), scalar1=-RW)
+            turned = psl.tile([P, 6, P], BF16, name="turned", tag="xl")
+            for k in range(2):
+                nc.tensor.transpose(turned[:, k, :], cols[:, k:256:2], identb[:])
+            for k in range(4):
+                nc.tensor.transpose(turned[:, 2 + k, :], cols[:, k:512:4], identb[:])
+            fps = {0: [hidden_row(0, c) for c in range(2)]}
+            pos = const.tile([P, 6, 14], F32)
+            nc.vector.tensor_copy(out=pos[:], in_=turned[:, :, 0:14])
+            hp2 = const.tile([P, 2, 8], F32)
+            nc.vector.tensor_scalar_mul(out=hp2[:], in0=pos[:, 0:2, 0:8], scalar1=2.0 * RW)
+            hp1 = const.tile([P, 2, 8], F32)
+            nc.vector.tensor_scalar_mul(out=hp1[:], in0=pos[:, 0:2, 0:8], scalar1=RW)
+            sop = const.tile([P, 2, 4], F32)
+            nc.vector.tensor_scalar_mul(out=sop[:], in0=pos[:, 0:2, 8:12], scalar1=-RW)
             beta = const.tile([P, 1], F32)
             nc.vector.tensor_scalar_mul(out=beta[:], in0=one[:], scalar1=KAP * BETA - 1.0)
-            ipf = const.tile([P, 4, 2], F32)
-            nc.vector.tensor_copy(out=ipf[:], in_=ipos[:])
-            bi = const.tile([P, 4], F32)
-            nc.vector.tensor_tensor(out=bi[:], in0=ipf[:, :, 0], in1=ipf[:, :, 1], op=ALU.add)
+            bi = const.tile([P, 2, 2], F32)
+            posi = pos[:, 2:6, 12:14].rearrange("p (e c) u -> p c e u", c=2)
+            nc.vector.tensor_tensor(out=bi[:], in0=posi[:, 0], in1=posi[:, 1], op=ALU.add)
             nc.vector.tensor_scalar(
                 out=bi[:], in0=bi[:], scalar1=-KAP * RW, scalar2=KAP * BETA - 1.0, op0=ALU.mult, op1=ALU.add
             )
@@ -183,10 +186,10 @@ def tile_physicalneuralnetwork_kernel(
             parts = {}
 
             def part_v(hh, g, c):
-                col = 2 * (4 * hh + g) + c
+                a = 4 * hh + g
                 t = pl.tile([P, 512], F32, name="pv", bufs=16)
                 nc.vector.tensor_scalar(
-                    out=t[:], in0=ixy[c][:], scalar1=hp2[:, col : col + 1], scalar2=hp1[:, col : col + 1],
+                    out=t[:], in0=ixy[c][:], scalar1=hp2[:, c, a : a + 1], scalar2=hp1[:, c, a : a + 1],
                     op0=ALU.max, op1=ALU.subtract,
                 )
                 parts[1, hh, g, c] = t
@@ -194,7 +197,7 @@ def tile_physicalneuralnetwork_kernel(
             def part_s(hh, g, c):
                 t = pl.tile([P, 512], F32, name="ps", bufs=16)
                 nc.scalar.activation(
-                    out=t[:], in_=fps[hh][c][:], func=ACT.Abs, bias=sop[:, 2 * g + c : 2 * g + c + 1], scale=RW
+                    out=t[:], in_=fps[hh][c][:], func=ACT.Abs, bias=sop[:, c, g : g + 1], scale=RW
                 )
                 parts[2, hh, g, c] = t
 
@@ -214,7 +217,7 @@ def tile_physicalneuralnetwork_kernel(
 
             def log(layer, hh, t):
                 if layer == 1:
-                    lv, bias = ll1[:, t, 512 * hh : 512 * hh + 512], bi[:, t : t + 1]
+                    lv, bias = ll1[:, t, 512 * hh : 512 * hh + 512], bi[:, t % 2, t // 2 : t // 2 + 1]
                 else:
                     lv, bias = ll2[:, 4 * hh + t, :], beta[:]
                 nc.scalar.activation(out=lv, in_=sums[layer, hh, t][:], func=ACT.Ln, bias=bias, scale=KAP)
@@ -228,33 +231,35 @@ def tile_physicalneuralnetwork_kernel(
                     part_v(0, g, c)
             clamp(1, 1)
             total(1, 0, 0)
-            fps[1] = [spread(psp, rowh[:, 1024:2048:2], "fp", "fx")]
-            b2p = spread(psx, rowb[:], "b2p", "xt")
+            fps[1] = [hidden_row(1, 0)]
+            b2p = spread(psx, biases[:], 8, "b2p", "xt")
+            b1t = psx.tile([P, P], BF16, name="b1t", tag="xt")
+            nc.tensor.transpose(b1t[:], biases[:, 0:P], identb[:])
             for g in range(4):
                 part_s(0, g, 1)
             for t in range(1, 4):
                 total(1, 0, t)
-            fps[1].append(spread(psp, rowh[:, 1025:2048:2], "fp", "fy"))
+            fps[1].append(hidden_row(1, 1))
             for g in range(4):
                 for c in range(2):
                     part_v(1, g, c)
             clamp(2, 0)
             clamp(2, 1)
+            nc.vector.tensor_copy(out=b2b[:], in_=b2p[:])
+            b1f = const.tile([P, 8], F32)
+            nc.vector.tensor_copy(out=b1f[:], in_=b1t[:, 0:8])
             for t in range(4):
                 log(1, 0, t)
                 part_s(1, t, 0)
                 total(2, 0, t)
             for q in range(4):
                 numer(u1, wc1, w1sb, q)
-            nc.vector.tensor_copy(out=b2b[:], in_=b2p[:])
             transposes(0)
             for t in range(4):
                 log(2, 0, t)
                 part_s(1, t, 1)
                 total(1, 1, t)
             transposes(1)
-            b1f = const.tile([P, 8], F32)
-            nc.vector.tensor_copy(out=b1f[:], in_=b1sb[:])
             copy_x(0, False)
             numer(u2, wc2, w2sb, 0)
             copy_x(1, False)

@@ -203,17 +203,19 @@ def tile_physicalneuralnetwork_kernel(
 
             sums = {}
 
-            def total(layer, hh, t):
-                xl = psl.tile([P, 4, P], F32, name="xl")
-                wcv = wc1[:, t, 512 * hh : 512 * hh + 512] if layer == 1 else wc2[:, 4 * hh + t, :]
-                nc.tensor.matmul(out=xl[:], lhsT=identb[:], rhs=wcv, start=True, stop=False)
-                for g in range(4):
-                    for c in range(2):
-                        nc.tensor.matmul(
-                            out=xl[:, g, :], lhsT=parts[layer, hh, g, c][:, P * t : P * t + P], rhs=ident[:],
-                            is_transpose=True, start=False, stop=(g == 3 and c == 1),
-                        )
-                sums[layer, hh, t] = xl
+            def totals(layer, hh, pair):
+                for t in pair:
+                    xl = psl.tile([P, 4, P], F32, name="xl")
+                    wcv = wc1[:, t, 512 * hh : 512 * hh + 512] if layer == 1 else wc2[:, 4 * hh + t, :]
+                    nc.tensor.matmul(out=xl[:], lhsT=identb[:], rhs=wcv, start=True, stop=False)
+                    sums[layer, hh, t] = xl
+                for t in pair:
+                    for g in range(4):
+                        for c in range(2):
+                            nc.tensor.matmul(
+                                out=sums[layer, hh, t][:, g, :], lhsT=parts[layer, hh, g, c][:, P * t : P * t + P],
+                                rhs=ident[:], is_transpose=True, start=False, stop=(g == 3 and c == 1),
+                            )
 
             def log(layer, hh, t):
                 if layer == 1:
@@ -230,15 +232,14 @@ def tile_physicalneuralnetwork_kernel(
                 for c in range(2):
                     part_v(0, g, c)
             clamp(1, 1)
-            total(1, 0, 0)
             fps[1] = [hidden_row(1, 0)]
             b2p = spread(psx, biases[:], 8, "b2p", "xt")
             b1t = psx.tile([P, P], BF16, name="b1t", tag="xt")
             nc.tensor.transpose(b1t[:], biases[:, 0:P], identb[:])
+            totals(1, 0, (0, 1))
             for g in range(4):
                 part_s(0, g, 1)
-            for t in range(1, 4):
-                total(1, 0, t)
+            totals(1, 0, (2, 3))
             fps[1].append(hidden_row(1, 1))
             for g in range(4):
                 for c in range(2):
@@ -251,15 +252,17 @@ def tile_physicalneuralnetwork_kernel(
             for t in range(4):
                 log(1, 0, t)
                 part_s(1, t, 0)
-                total(2, 0, t)
+                if t % 2:
+                    totals(2, 0, (t - 1, t))
             for q in range(4):
                 numer(u1, wc1, w1sb, q)
             transposes(0)
+            transposes(1)
             for t in range(4):
                 log(2, 0, t)
                 part_s(1, t, 1)
-                total(1, 1, t)
-            transposes(1)
+                if t % 2:
+                    totals(1, 1, (t - 1, t))
             copy_x(0, False)
             numer(u2, wc2, w2sb, 0)
             copy_x(1, False)
@@ -269,7 +272,8 @@ def tile_physicalneuralnetwork_kernel(
             numer(u2, wc2, w2sb, 3)
             for t in range(4):
                 log(1, 1, t)
-                total(2, 1, t)
+                if t % 2:
+                    totals(2, 1, (t - 1, t))
             for t in range(4):
                 log(2, 1, t)
             for pair in (2, 3):

@@ -28,7 +28,6 @@ def tile_physicalneuralnetwork_kernel(
     with ExitStack() as ctx:
         const = ctx.enter_context(tc.tile_pool(name="const", bufs=1))
         w8 = ctx.enter_context(tc.tile_pool(name="w8", bufs=2))
-        psx = ctx.enter_context(tc.psum_pool(name="psx", bufs=2))
         ctx.enter_context(tc.manual_schedule())
         ctx.enter_context(nc.allow_non_contiguous_dma(reason="small per-partition vectors"))
 
@@ -98,7 +97,7 @@ def tile_physicalneuralnetwork_kernel(
         xts = {}
 
         def transposes(pair):
-            xt = psx.tile([P, 2, 2, P], F32, name="xt")
+            xt = psx[0].tile([P, 2, 2, P], F32, name="xt", tag="xl")
             for rr in range(2):
                 xw = xsb[:, 2 * pair + rr, :].bitcast(F32)
                 for u in range(2):
@@ -137,7 +136,8 @@ def tile_physicalneuralnetwork_kernel(
                 in_=e[:, k].rearrange("p h t -> p (h t)"),
             )
 
-        with tc.psum_pool(name="psp", bufs=1) as psp, tc.psum_pool(name="psl", bufs=4) as psl, tc.tile_pool(
+        psx = {}
+        with tc.psum_pool(name="psp", bufs=1) as psp, tc.psum_pool(name="psl", bufs=6) as psl, tc.tile_pool(
             name="pl", bufs=8
         ) as pl:
             def spread(pool, src, row, name, tag):
@@ -154,7 +154,7 @@ def tile_physicalneuralnetwork_kernel(
             warm = const.tile([P, 1], F32)
             nc.scalar.activation(out=warm[:], in_=one[:], func=ACT.Ln)
             ixy = []
-            ips = [spread(psx, iv[:, c], 0, "ip", "xt") for c in range(2)]
+            ips = [spread(psl, iv[:, c], 0, "ip", "xl") for c in range(2)]
             for c in range(2):
                 it = const.tile([P, 512], F32, name="i" + "xy"[c])
                 nc.scalar.activation(out=it[:], in_=ips[c][:], func=ACT.Copy, scale=2.0 * RW)
@@ -183,6 +183,7 @@ def tile_physicalneuralnetwork_kernel(
                 out=bi[:], in0=bi[:], scalar1=-KAP * RW, scalar2=KAP * BETA - 1.0, op0=ALU.mult, op1=ALU.add
             )
 
+            psx[0] = psl
             parts = {}
 
             def part_v(hh, g, c):
@@ -203,13 +204,13 @@ def tile_physicalneuralnetwork_kernel(
 
             sums = {}
 
-            def totals(layer, hh, pair):
-                for t in pair:
+            def totals(layer, hh):
+                for t in range(4):
                     xl = psl.tile([P, 4, P], F32, name="xl")
                     wcv = wc1[:, t, 512 * hh : 512 * hh + 512] if layer == 1 else wc2[:, 4 * hh + t, :]
                     nc.tensor.matmul(out=xl[:], lhsT=identb[:], rhs=wcv, start=True, stop=False)
                     sums[layer, hh, t] = xl
-                for t in pair:
+                for t in range(4):
                     for g in range(4):
                         for c in range(2):
                             nc.tensor.matmul(
@@ -231,56 +232,50 @@ def tile_physicalneuralnetwork_kernel(
             for g in range(4):
                 for c in range(2):
                     part_v(0, g, c)
-            clamp(1, 1)
+                if g == 1:
+                    clamp(1, 1)
             fps[1] = [hidden_row(1, 0)]
-            b2p = spread(psx, biases[:], 8, "b2p", "xt")
-            b1t = psx.tile([P, P], BF16, name="b1t", tag="xt")
-            nc.tensor.transpose(b1t[:], biases[:, 0:P], identb[:])
-            totals(1, 0, (0, 1))
+            totals(1, 0)
             for g in range(4):
                 part_s(0, g, 1)
-            totals(1, 0, (2, 3))
             fps[1].append(hidden_row(1, 1))
+            clamp(2, 0)
+            clamp(2, 1)
             for g in range(4):
                 for c in range(2):
                     part_v(1, g, c)
-            clamp(2, 0)
-            clamp(2, 1)
+            for t in range(4):
+                log(1, 0, t)
+            totals(2, 0)
+            for g in range(4):
+                part_s(1, g, 0)
+            for q in range(4):
+                numer(u1, wc1, w1sb, q)
+            for t in range(4):
+                log(2, 0, t)
+            for g in range(4):
+                part_s(1, g, 1)
+            totals(1, 1)
+            for q in range(4):
+                numer(u2, wc2, w2sb, q)
+            for t in range(4):
+                log(1, 1, t)
+            b2p = spread(psl, biases[:], 8, "b2p", "xl")
+            totals(2, 1)
+            b1t = psl.tile([P, P], BF16, name="b1t", tag="xl")
+            nc.tensor.transpose(b1t[:], biases[:, 0:P], identb[:])
             nc.vector.tensor_copy(out=b2b[:], in_=b2p[:])
             b1f = const.tile([P, 8], F32)
             nc.vector.tensor_copy(out=b1f[:], in_=b1t[:, 0:8])
             for t in range(4):
-                log(1, 0, t)
-                part_s(1, t, 0)
-                if t % 2:
-                    totals(2, 0, (t - 1, t))
-            for q in range(4):
-                numer(u1, wc1, w1sb, q)
-            transposes(0)
-            transposes(1)
-            for t in range(4):
-                log(2, 0, t)
-                part_s(1, t, 1)
-                if t % 2:
-                    totals(1, 1, (t - 1, t))
-            copy_x(0, False)
-            numer(u2, wc2, w2sb, 0)
-            copy_x(1, False)
-            numer(u2, wc2, w2sb, 1)
-            quant_x(0)
-            numer(u2, wc2, w2sb, 2)
-            numer(u2, wc2, w2sb, 3)
-            for t in range(4):
-                log(1, 1, t)
-                if t % 2:
-                    totals(2, 1, (t - 1, t))
-            for t in range(4):
                 log(2, 1, t)
-            for pair in (2, 3):
+            for pair in range(4):
                 transposes(pair)
                 copy_x(pair, False)
+            quant_x(0)
             quant_x(1)
 
+        psx[0] = ctx.enter_context(tc.psum_pool(name="psx", bufs=2))
         psa = ctx.enter_context(tc.psum_pool(name="psa", bufs=4))
         psb = ctx.enter_context(tc.psum_pool(name="psb", bufs=2))
         hp = ctx.enter_context(tc.tile_pool(name="hp", bufs=2))

@@ -1,3 +1,4 @@
+import itertools
 from contextlib import ExitStack
 
 import concourse.mybir as mybir
@@ -204,19 +205,33 @@ def tile_physicalneuralnetwork_kernel(
 
             sums = {}
 
-            def totals(layer, hh):
-                for t in range(4):
-                    xl = psl.tile([P, 4, P], F32, name="xl")
+            def totals(layer, hh, blocks, clip_first):
+                for t in blocks:
+                    sums[layer, hh, t] = psl.tile([P, 4, P], F32, name="xl")
+
+                def turn(t, g, c):
+                    first, last = g == 0 and c == 0, g == 3 and c == 1
+                    nc.tensor.matmul(
+                        out=sums[layer, hh, t][:, g, :], lhsT=parts[layer, hh, g, c][:, P * t : P * t + P],
+                        rhs=ident[:], is_transpose=True, start=first and not clip_first, stop=last and clip_first,
+                    )
+
+                def add_clip(t):
                     wcv = wc1[:, t, 512 * hh : 512 * hh + 512] if layer == 1 else wc2[:, 4 * hh + t, :]
-                    nc.tensor.matmul(out=xl[:], lhsT=identb[:], rhs=wcv, start=True, stop=False)
-                    sums[layer, hh, t] = xl
-                for t in range(4):
-                    for g in range(4):
-                        for c in range(2):
-                            nc.tensor.matmul(
-                                out=sums[layer, hh, t][:, g, :], lhsT=parts[layer, hh, g, c][:, P * t : P * t + P],
-                                rhs=ident[:], is_transpose=True, start=False, stop=(g == 3 and c == 1),
-                            )
+                    nc.tensor.matmul(
+                        out=sums[layer, hh, t][:], lhsT=identb[:], rhs=wcv, start=clip_first, stop=not clip_first
+                    )
+
+                if clip_first:
+                    for t in blocks:
+                        add_clip(t)
+                    for t, g, c in itertools.product(blocks, range(4), range(2)):
+                        turn(t, g, c)
+                else:
+                    for g, c, t in itertools.product(range(4), range(2), blocks):
+                        turn(t, g, c)
+                    for t in blocks:
+                        add_clip(t)
 
             def log(layer, hh, t):
                 if layer == 1:
@@ -228,52 +243,54 @@ def tile_physicalneuralnetwork_kernel(
             b2b = const.tile([P, O], F32)
             for g in range(4):
                 part_s(0, g, 0)
-            clamp(1, 0)
             for g in range(4):
                 for c in range(2):
                     part_v(0, g, c)
-                if g == 1:
-                    clamp(1, 1)
-            fps[1] = [hidden_row(1, 0)]
-            totals(1, 0)
+            clamp(1, 0)
+            clamp(1, 1)
+            totals(1, 0, range(4), False)
             for g in range(4):
                 part_s(0, g, 1)
-            fps[1].append(hidden_row(1, 1))
+            for t in range(4):
+                log(1, 0, t)
+            fps[1] = [hidden_row(1, c) for c in range(2)]
             clamp(2, 0)
             clamp(2, 1)
+            totals(2, 0, range(4), True)
+            transposes(0)
+            transposes(1)
             for g in range(4):
                 for c in range(2):
                     part_v(1, g, c)
             for t in range(4):
-                log(1, 0, t)
-            totals(2, 0)
-            for g in range(4):
-                part_s(1, g, 0)
-            for q in range(4):
-                numer(u1, wc1, w1sb, q)
-            for t in range(4):
                 log(2, 0, t)
-            for g in range(4):
-                part_s(1, g, 1)
-            totals(1, 1)
-            for q in range(4):
-                numer(u2, wc2, w2sb, q)
+            for c, g in itertools.product(range(2), range(4)):
+                part_s(1, g, c)
+            numer(u1, wc1, w1sb, 0)
+            copy_x(0, False)
+            copy_x(1, False)
+            for q in range(1, 4):
+                numer(u1, wc1, w1sb, q)
+            quant_x(0)
+            totals(1, 1, range(4), False)
             for t in range(4):
                 log(1, 1, t)
-            b2p = spread(psl, biases[:], 8, "b2p", "xl")
-            totals(2, 1)
-            b1t = psl.tile([P, P], BF16, name="b1t", tag="xl")
-            nc.tensor.transpose(b1t[:], biases[:, 0:P], identb[:])
-            nc.vector.tensor_copy(out=b2b[:], in_=b2p[:])
-            b1f = const.tile([P, 8], F32)
-            nc.vector.tensor_copy(out=b1f[:], in_=b1t[:, 0:8])
+            for q in range(4):
+                numer(u2, wc2, w2sb, q)
+            totals(2, 1, range(0, 2), True)
+            totals(2, 1, range(2, 4), True)
             for t in range(4):
                 log(2, 1, t)
-            for pair in range(4):
+            for pair in (2, 3):
                 transposes(pair)
                 copy_x(pair, False)
-            quant_x(0)
+            b1t = psl.tile([P, P], BF16, name="b1t", tag="xl")
+            nc.tensor.transpose(b1t[:], biases[:, 0:P], identb[:])
+            b2p = spread(psl, biases[:], 8, "b2p", "xl")
             quant_x(1)
+            b1f = const.tile([P, 8], F32)
+            nc.vector.tensor_copy(out=b1f[:], in_=b1t[:, 0:8])
+            nc.vector.tensor_copy(out=b2b[:], in_=b2p[:])
 
         psx[0] = ctx.enter_context(tc.psum_pool(name="psx", bufs=2))
         psa = ctx.enter_context(tc.psum_pool(name="psa", bufs=4))

@@ -32,18 +32,13 @@ def tile_physicalneuralnetwork_kernel(
         ctx.enter_context(tc.manual_schedule())
         ctx.enter_context(nc.allow_non_contiguous_dma(reason="small per-partition vectors"))
 
-        rows = const.tile([P, 1024], BF16)
-        nc.vector.memset(rows[:].bitcast(U32)[:, 0:256], 0)
-        nc.gpsimd.memset(rows[:].bitcast(U32)[:, 256:512], 0)
+        rows = const.tile([P, 512], BF16)
+        nc.vector.memset(rows[:].bitcast(U32), 0)
         one = const.tile([P, 1], F32)
         nc.vector.memset(one[:], 1.0)
-        cols = const.tile([P, 512], BF16)
-        nc.vector.memset(cols[:].bitcast(U32), 0)
-        nc.sync.dma_start(out=rows[0:1, :], in_=input_positions.rearrange("(a h) c -> a (h c)", a=1))
-        nc.sync.dma_start(out=rows[1:3, :], in_=hidden_positions.rearrange("(a h) c -> a (h c)", a=2))
-        nc.sync.dma_start(out=cols[0:8, 0:256], in_=hidden_positions.rearrange("(a p) c -> a (p c)", p=P))
-        nc.sync.dma_start(out=cols[8:12, 0:256], in_=output_positions.rearrange("(a p) c -> a (p c)", p=P))
-        nc.sync.dma_start(out=cols[12:14, 0:512], in_=input_positions.rearrange("(u r) c -> u (r c)", u=2))
+        nc.sync.dma_start(out=rows[0:2, :], in_=input_positions.rearrange("(u r) c -> u (r c)", u=2))
+        nc.sync.dma_start(out=rows[2:10, 0:256], in_=hidden_positions.rearrange("(a p) c -> a (p c)", p=P))
+        nc.sync.dma_start(out=rows[10:14, 0:256], in_=output_positions.rearrange("(a p) c -> a (p c)", p=P))
         w1sb = const.tile([P, 4, H], BF16)
         for u in range(2):
             nc.sync.dma_start(
@@ -123,9 +118,9 @@ def tile_physicalneuralnetwork_kernel(
         def recip(lv):
             nc.scalar.activation(out=lv, in_=lv, func=ACT.Sigmoid, scale=-1.0)
 
-        def eff(e, uv, lv, k):
+        def eff(ev, uv, lv):
             nc.vector.tensor_tensor(
-                out=e[:, k].rearrange("p (c i) t -> p c t i", i=4),
+                out=ev.rearrange("p (c i) t -> p c t i", i=4),
                 in0=uv.rearrange("p t (c i) -> p c t i", i=4),
                 in1=lv.rearrange("p t (c i) -> p c t i", i=4), op=ALU.mult,
             )
@@ -141,49 +136,59 @@ def tile_physicalneuralnetwork_kernel(
         with tc.psum_pool(name="psp", bufs=1) as psp, tc.psum_pool(name="psl", bufs=6) as psl, tc.tile_pool(
             name="pl", bufs=8
         ) as pl:
-            def spread(pool, src, row, name, tag):
-                t = pool.tile([P, 512], F32, name=name, tag=tag)
+            def spread(out, row, src):
                 nc.tensor.matmul(
-                    out=t[:], lhsT=identb[:, row : row + 1].to_broadcast([P, P]), rhs=src, start=True, stop=True
+                    out=out, lhsT=identb[:, row : row + 1].to_broadcast([P, P]), rhs=src, start=True, stop=True
                 )
-                return t
 
             def hidden_row(hh, c):
-                return spread(psp, rows[:, c:1024:2], 1 + hh, "fp", "f" + "xy"[c])
+                t = psp.tile([P, 4, P], F32, name="fp", tag="f" + "xy"[c])
+                for g in range(4):
+                    spread(t[:, g], 2 + 4 * hh + g, rows[:, c:256:2])
+                return t
 
-            iv = rows[:].rearrange("k (u p e c) -> k c u e p", u=2, p=P, e=2, c=2)
+            def input_row(c):
+                t = psl.tile([P, 4, P], F32, name="ip", tag="xl")
+                for k in range(4):
+                    spread(t[:, k], k // 2, rows[:, 2 * (k % 2) + c : 512 : 4])
+                return t
+
             warm = const.tile([P, 1], F32)
             nc.scalar.activation(out=warm[:], in_=one[:], func=ACT.Ln)
-            ixy = []
-            ips = [spread(psl, iv[:, c], 0, "ip", "xl") for c in range(2)]
-            for c in range(2):
-                it = const.tile([P, 512], F32, name="i" + "xy"[c])
-                nc.scalar.activation(out=it[:], in_=ips[c][:], func=ACT.Copy, scale=2.0 * RW)
-                ixy.append(it)
 
             turned = psl.tile([P, 6, P], BF16, name="turned", tag="xl")
             for k in range(2):
-                nc.tensor.transpose(turned[:, k, :], cols[:, k:256:2], identb[:])
+                nc.tensor.transpose(turned[:, k, :], rows[:, k:256:2], identb[:])
             for k in range(4):
-                nc.tensor.transpose(turned[:, 2 + k, :], cols[:, k:512:4], identb[:])
+                nc.tensor.transpose(turned[:, 2 + k, :], rows[:, k:512:4], identb[:])
+            ips = [input_row(c) for c in range(2)]
             fps = {0: [hidden_row(0, c) for c in range(2)]}
             pos = const.tile([P, 6, 14], F32)
             nc.vector.tensor_copy(out=pos[:], in_=turned[:, :, 0:14])
-            hp2 = const.tile([P, 2, 8], F32)
-            nc.vector.tensor_scalar_mul(out=hp2[:], in0=pos[:, 0:2, 0:8], scalar1=2.0 * RW)
-            hp1 = const.tile([P, 2, 8], F32)
-            nc.vector.tensor_scalar_mul(out=hp1[:], in0=pos[:, 0:2, 0:8], scalar1=RW)
             sop = const.tile([P, 2, 4], F32)
-            nc.vector.tensor_scalar_mul(out=sop[:], in0=pos[:, 0:2, 8:12], scalar1=-RW)
-            beta = const.tile([P, 1], F32)
-            nc.vector.tensor_scalar_mul(out=beta[:], in0=one[:], scalar1=KAP * BETA - 1.0)
-            bi = const.tile([P, 2, 2], F32)
-            posi = pos[:, 2:6, 12:14].rearrange("p (e c) u -> p c e u", c=2)
-            nc.vector.tensor_tensor(out=bi[:], in0=posi[:, 0], in1=posi[:, 1], op=ALU.add)
-            nc.vector.tensor_scalar(
-                out=bi[:], in0=bi[:], scalar1=-KAP * RW, scalar2=KAP * BETA - 1.0, op0=ALU.mult, op1=ALU.add
-            )
+            nc.vector.tensor_scalar_mul(out=sop[:], in0=pos[:, 0:2, 10:14], scalar1=-RW)
+            hp2 = const.tile([P, 2, 8], F32)
+            nc.vector.tensor_scalar_mul(out=hp2[:], in0=pos[:, 0:2, 2:10], scalar1=2.0 * RW)
+            hp1 = const.tile([P, 2, 8], F32)
+            nc.vector.tensor_scalar_mul(out=hp1[:], in0=pos[:, 0:2, 2:10], scalar1=RW)
+            ixy = []
+            for c in range(2):
+                it = const.tile([P, 512], F32, name="i" + "xy"[c])
+                nc.scalar.activation(
+                    out=it[:], in_=ips[c][:].rearrange("p t n -> p (t n)"), func=ACT.Copy, scale=2.0 * RW
+                )
+                ixy.append(it)
 
+            def input_biases():
+                nc.vector.tensor_scalar_mul(out=beta[:], in0=one[:], scalar1=KAP * BETA - 1.0)
+                posi = pos[:, 2:6, 0:2].rearrange("p (e c) u -> p c e u", c=2)
+                nc.vector.tensor_tensor(out=bi[:], in0=posi[:, 0], in1=posi[:, 1], op=ALU.add)
+                nc.vector.tensor_scalar(
+                    out=bi[:], in0=bi[:], scalar1=-KAP * RW, scalar2=KAP * BETA - 1.0, op0=ALU.mult, op1=ALU.add
+                )
+
+            beta = const.tile([P, 1], F32)
+            bi = const.tile([P, 2, 2], F32)
             psx[0] = psl
             parts = {}
 
@@ -199,7 +204,7 @@ def tile_physicalneuralnetwork_kernel(
             def part_s(hh, g, c):
                 t = pl.tile([P, 512], F32, name="ps", bufs=16)
                 nc.scalar.activation(
-                    out=t[:], in_=fps[hh][c][:], func=ACT.Abs, bias=sop[:, c, g : g + 1], scale=RW
+                    out=t[:], in_=fps[hh][c][:].rearrange("p g n -> p (g n)"), func=ACT.Abs, bias=sop[:, c, g : g + 1], scale=RW
                 )
                 parts[2, hh, g, c] = t
 
@@ -225,10 +230,10 @@ def tile_physicalneuralnetwork_kernel(
                 if clip_first:
                     for t in blocks:
                         add_clip(t)
-                    for t, g, c in itertools.product(blocks, range(4), range(2)):
+                    for t, c, g in itertools.product(blocks, range(2), range(4)):
                         turn(t, g, c)
                 else:
-                    for g, c, t in itertools.product(range(4), range(2), blocks):
+                    for c, g, t in itertools.product(range(2), range(4), blocks):
                         turn(t, g, c)
                     for t in blocks:
                         add_clip(t)
@@ -241,16 +246,14 @@ def tile_physicalneuralnetwork_kernel(
                 nc.scalar.activation(out=lv, in_=sums[layer, hh, t][:], func=ACT.Ln, bias=bias, scale=KAP)
 
             b2b = const.tile([P, O], F32)
-            for g in range(4):
-                part_s(0, g, 0)
-            for g in range(4):
-                for c in range(2):
-                    part_v(0, g, c)
+            for c, g in itertools.product(range(2), range(4)):
+                part_s(0, g, c)
+            for c, g in itertools.product(range(2), range(4)):
+                part_v(0, g, c)
+            input_biases()
             clamp(1, 0)
             clamp(1, 1)
             totals(1, 0, range(4), False)
-            for g in range(4):
-                part_s(0, g, 1)
             for t in range(4):
                 log(1, 0, t)
             fps[1] = [hidden_row(1, c) for c in range(2)]
@@ -259,18 +262,18 @@ def tile_physicalneuralnetwork_kernel(
             totals(2, 0, range(4), True)
             transposes(0)
             transposes(1)
-            for g in range(4):
-                for c in range(2):
-                    part_v(1, g, c)
+            for c, g in itertools.product(range(2), range(4)):
+                part_v(1, g, c)
             for t in range(4):
                 log(2, 0, t)
             for c, g in itertools.product(range(2), range(4)):
                 part_s(1, g, c)
             numer(u1, wc1, w1sb, 0)
+            numer(u1, wc1, w1sb, 1)
             copy_x(0, False)
             copy_x(1, False)
-            for q in range(1, 4):
-                numer(u1, wc1, w1sb, q)
+            numer(u1, wc1, w1sb, 2)
+            numer(u1, wc1, w1sb, 3)
             quant_x(0)
             totals(1, 1, range(4), False)
             for t in range(4):
@@ -286,15 +289,16 @@ def tile_physicalneuralnetwork_kernel(
                 copy_x(pair, False)
             b1t = psl.tile([P, P], BF16, name="b1t", tag="xl")
             nc.tensor.transpose(b1t[:], biases[:, 0:P], identb[:])
-            b2p = spread(psl, biases[:], 8, "b2p", "xl")
+            b2p = psl.tile([P, O], F32, name="b2p", tag="xl")
+            spread(b2p[:], 8, biases[:])
             quant_x(1)
             b1f = const.tile([P, 8], F32)
             nc.vector.tensor_copy(out=b1f[:], in_=b1t[:, 0:8])
             nc.vector.tensor_copy(out=b2b[:], in_=b2p[:])
 
-        psx[0] = ctx.enter_context(tc.psum_pool(name="psx", bufs=2))
         psa = ctx.enter_context(tc.psum_pool(name="psa", bufs=4))
-        psb = ctx.enter_context(tc.psum_pool(name="psb", bufs=2))
+        psb = ctx.enter_context(tc.psum_pool(name="psb", bufs=4))
+        psx[0] = psb
         hp = ctx.enter_context(tc.tile_pool(name="hp", bufs=2))
         hq = ctx.enter_context(tc.tile_pool(name="hq", bufs=3))
         op = ctx.enter_context(tc.tile_pool(name="op", bufs=10))
@@ -306,12 +310,12 @@ def tile_physicalneuralnetwork_kernel(
             g, oh = k // 2, k % 2
             return t[:, 4 * g : 4 * g + 4, CH * oh : CH * oh + CH]
 
-        def eff1(k):
-            cols = slice(CH * k, CH * k + CH)
-            eff(e1, u1[:, :, cols], ll1[:, :, cols], k)
+        def eff1(lo, n):
+            cols = slice(lo, lo + n)
+            eff(e1[:].rearrange("p k n t -> p (k n) t")[:, cols], u1[:, :, cols], ll1[:, :, cols])
 
         def eff2(k):
-            eff(e2, view2(u2, k), view2(ll2, k), k)
+            eff(e2[:, k], view2(u2, k), view2(ll2, k))
 
         ov = out.rearrange("(m r) o -> m r o", r=16)
         hid = {}
@@ -355,7 +359,7 @@ def tile_physicalneuralnetwork_kernel(
 
         def l2_mm(c, rr):
             cc, sc = hid[c][2], hid[c][3]
-            ps2 = psb.tile([P, 512], F32, name="ps2")
+            ps2 = psb.tile([P, 512], F32, name="ps2", tag="xl")
             for g in range(2):
                 nc.tensor.matmul_mx(
                     out=ps2[:],
@@ -376,14 +380,18 @@ def tile_physicalneuralnetwork_kernel(
             nc.scalar.activation(out=ot[:], in_=ot[:], func=ACT.Sigmoid)
             nc.sync.dma_start(out=ov[:, 4 * c + rr, :], in_=ot[:])
 
-        for k in range(4):
-            recip(ll1[:, :, CH * k : CH * k + CH])
+        pieces = [(0, CH // 2), (CH // 2, CH // 2)] + [(CH * k, CH) for k in range(1, 4)]
+        for lo, n in pieces:
+            recip(ll1[:, :, lo : lo + n])
         for k in range(4):
             recip(view2(ll2, k))
-        for k in range(4):
-            eff1(k)
-            if k > 0:
-                quant_w(e1, c1, s1, k - 1)
+        eff1(*pieces[0])
+        eff1(*pieces[1])
+        quant_w(e1, c1, s1, 0)
+        eff1(*pieces[2])
+        for k in range(1, 3):
+            eff1(*pieces[k + 2])
+            quant_w(e1, c1, s1, k)
         eff2(0)
         quant_w(e1, c1, s1, 3)
         for k in range(1, 4):
@@ -403,28 +411,29 @@ def tile_physicalneuralnetwork_kernel(
         for pair in (6, 7):
             transposes(pair)
             copy_x(pair, True)
-        l1_mm(2, range(0, 2))
         regroup(1, 0)
         l2_mm(0, 0)
         l2_mm(0, 1)
+        l1_mm(2, range(0, 4))
         regroup(1, 1)
         quant_h(1, 0)
         quant_x(3)
         l2_mm(0, 2)
         l2_mm(0, 3)
         quant_h(1, 1)
-        l1_mm(2, range(2, 8))
+        l1_mm(2, range(4, 8))
         for rr in range(4):
             l2_out(0, rr)
         regroup(2, 0)
         l2_mm(1, 0)
         l2_mm(1, 1)
+        l1_mm(3, range(0, 4))
         regroup(2, 1)
         l2_mm(1, 2)
         l2_mm(1, 3)
-        l1_mm(3, range(0, 8))
         quant_h(2, 0)
         quant_h(2, 1)
+        l1_mm(3, range(4, 8))
         for rr in range(4):
             l2_out(1, rr)
         regroup(3, 0)

@@ -357,23 +357,35 @@ def tile_physicalneuralnetwork_kernel(
 
         outs = {}
 
-        def l2_mm(c, rr):
+        sums2 = {}
+
+        def l2_pass(c, rr, g):
             cc, sc = hid[c][2], hid[c][3]
-            ps2 = psb.tile([P, 512], F32, name="ps2", tag="xl")
-            for g in range(2):
-                nc.tensor.matmul_mx(
-                    out=ps2[:],
-                    lhsT=cc[:, g, P * rr : P * rr + P].bitcast(FP8X4),
-                    lhsT_scale=sc[:, g, P * rr : P * rr + P],
-                    rhs=c2[:, 512 * g : 512 * g + 512].bitcast(FP8X4),
-                    rhs_scale=s2[:, 512 * g : 512 * g + 512],
-                    start=(g == 0), stop=(g == 1),
+            if g == 0:
+                sums2[c, rr] = psa.tile([P, 512], F32, name="ps") if c == 3 else psb.tile(
+                    [P, 512], F32, name="ps2", tag="xl"
                 )
+            nc.tensor.matmul_mx(
+                out=sums2[c, rr][:],
+                lhsT=cc[:, g, P * rr : P * rr + P].bitcast(FP8X4),
+                lhsT_scale=sc[:, g, P * rr : P * rr + P],
+                rhs=c2[:, 512 * g : 512 * g + 512].bitcast(FP8X4),
+                rhs_scale=s2[:, 512 * g : 512 * g + 512],
+                start=(g == 0), stop=(g == 1),
+            )
+
+        def l2_add(c, rr):
+            ps2 = sums2[c, rr]
             ot = op.tile([P, 512], F32, name="ot")
             outs[(c, rr)] = ot
             nc.vector.scalar_tensor_tensor(
                 out=ot[:], in0=ps2[:], scalar=KAP, in1=b2b[:], op0=ALU.mult, op1=ALU.add
             )
+
+        def l2_mm(c, rr):
+            l2_pass(c, rr, 0)
+            l2_pass(c, rr, 1)
+            l2_add(c, rr)
 
         def l2_out(c, rr):
             ot = outs[(c, rr)]
@@ -405,15 +417,15 @@ def tile_physicalneuralnetwork_kernel(
         quant_w(e2, c2, s2, 3)
         regroup(0, 1)
         quant_h(0, 0)
-        quant_x(2)
         quant_h(0, 1)
+        quant_x(2)
         l1_mm(1, range(0, 8))
-        for pair in (6, 7):
-            transposes(pair)
-            copy_x(pair, True)
         regroup(1, 0)
         l2_mm(0, 0)
         l2_mm(0, 1)
+        for pair in (6, 7):
+            transposes(pair)
+            copy_x(pair, True)
         l1_mm(2, range(0, 4))
         regroup(1, 1)
         quant_h(1, 0)
@@ -440,12 +452,19 @@ def tile_physicalneuralnetwork_kernel(
         l2_mm(2, 0)
         l2_mm(2, 1)
         regroup(3, 1)
+        l2_pass(2, 2, 0)
+        l2_pass(2, 2, 1)
+        l2_pass(2, 3, 0)
+        l2_pass(2, 3, 1)
         quant_h(3, 0)
         quant_h(3, 1)
-        l2_mm(2, 2)
-        l2_mm(2, 3)
+        l2_add(2, 2)
+        l2_add(2, 3)
         for rr in range(4):
             l2_out(2, rr)
         for rr in range(4):
-            l2_mm(3, rr)
+            l2_pass(3, rr, 0)
+        for rr in range(4):
+            l2_pass(3, rr, 1)
+            l2_add(3, rr)
             l2_out(3, rr)

@@ -342,12 +342,18 @@ def tile_physicalneuralnetwork_kernel(
                     out=hc[:, mt, :], in_=ps[:], func=ACT.Sigmoid, bias=b1f[:, mt : mt + 1], scale=KAP
                 )
 
-        def regroup(c, g):
+        def regroup(c, g, on_gpsimd=False):
             hc, gc = hid[c][0], hid[c][1]
-            nc.vector.tensor_copy(
-                out=gc[:, g].rearrange("p (c i) t -> p c t i", i=4),
-                in_=hc[:, 4 * g : 4 * g + 4, :].rearrange("p t (c i) -> p c t i", i=4),
-            )
+            if on_gpsimd:
+                nc.gpsimd.tensor_scalar(
+                    out=gc[:, g], in0=hc[:, 4 * g : 4 * g + 4, :].rearrange("p t n -> p n t"), scalar1=1.0, scalar2=0.0,
+                    op0=ALU.mult, op1=ALU.add,
+                )
+            else:
+                nc.vector.tensor_copy(
+                    out=gc[:, g].rearrange("p (c i) t -> p c t i", i=4),
+                    in_=hc[:, 4 * g : 4 * g + 4, :].rearrange("p t (c i) -> p c t i", i=4),
+                )
 
         def quant_h(c, g):
             gc, cc, sc = hid[c][1], hid[c][2], hid[c][3]
@@ -374,13 +380,16 @@ def tile_physicalneuralnetwork_kernel(
                 start=(g == 0), stop=(g == 1),
             )
 
+        def out_columns(c, rr):
+            return (slice(0, 256), slice(256, 512)) if (c, rr) == (3, 3) else (slice(0, 512),)
+
         def l2_add(c, rr):
-            ps2 = sums2[c, rr]
             ot = op.tile([P, 512], F32, name="ot")
             outs[(c, rr)] = ot
-            nc.vector.scalar_tensor_tensor(
-                out=ot[:], in0=ps2[:], scalar=KAP, in1=b2b[:], op0=ALU.mult, op1=ALU.add
-            )
+            for cols in out_columns(c, rr):
+                nc.vector.scalar_tensor_tensor(
+                    out=ot[:, cols], in0=sums2[c, rr][:, cols], scalar=KAP, in1=b2b[:, cols], op0=ALU.mult, op1=ALU.add
+                )
 
         def l2_mm(c, rr):
             l2_pass(c, rr, 0)
@@ -389,8 +398,9 @@ def tile_physicalneuralnetwork_kernel(
 
         def l2_out(c, rr):
             ot = outs[(c, rr)]
-            nc.scalar.activation(out=ot[:], in_=ot[:], func=ACT.Sigmoid)
-            nc.sync.dma_start(out=ov[:, 4 * c + rr, :], in_=ot[:])
+            for cols in out_columns(c, rr):
+                nc.scalar.activation(out=ot[:, cols], in_=ot[:, cols], func=ACT.Sigmoid)
+                nc.sync.dma_start(out=ov[:, 4 * c + rr, cols], in_=ot[:, cols])
 
         pieces = [(0, CH // 2), (CH // 2, CH // 2)] + [(CH * k, CH) for k in range(1, 4)]
         for lo, n in pieces:
@@ -425,22 +435,23 @@ def tile_physicalneuralnetwork_kernel(
         l2_mm(0, 1)
         for pair in (6, 7):
             transposes(pair)
-            copy_x(pair, True)
+        regroup(1, 1, True)
         l1_mm(2, range(0, 4))
-        regroup(1, 1)
-        quant_h(1, 0)
-        quant_x(3)
+        for pair in (6, 7):
+            copy_x(pair, False)
         l2_mm(0, 2)
         l2_mm(0, 3)
+        quant_h(1, 0)
         quant_h(1, 1)
+        quant_x(3)
         l1_mm(2, range(4, 8))
         for rr in range(4):
             l2_out(0, rr)
         regroup(2, 0)
+        regroup(2, 1, True)
         l2_mm(1, 0)
         l2_mm(1, 1)
         l1_mm(3, range(0, 4))
-        regroup(2, 1)
         l2_mm(1, 2)
         l2_mm(1, 3)
         quant_h(2, 0)
@@ -450,20 +461,16 @@ def tile_physicalneuralnetwork_kernel(
             l2_out(1, rr)
         regroup(3, 0)
         l2_mm(2, 0)
+        quant_h(3, 0)
         l2_mm(2, 1)
         regroup(3, 1)
-        l2_pass(2, 2, 0)
-        l2_pass(2, 2, 1)
-        l2_pass(2, 3, 0)
-        l2_pass(2, 3, 1)
-        quant_h(3, 0)
-        quant_h(3, 1)
-        l2_add(2, 2)
-        l2_add(2, 3)
-        for rr in range(4):
-            l2_out(2, rr)
         for rr in range(4):
             l2_pass(3, rr, 0)
+        l2_mm(2, 2)
+        quant_h(3, 1)
+        l2_mm(2, 3)
+        for rr in range(4):
+            l2_out(2, rr)
         for rr in range(4):
             l2_pass(3, rr, 1)
             l2_add(3, rr)

@@ -156,14 +156,15 @@ def tile_physicalneuralnetwork_kernel(
             warm = const.tile([P, 1], F32)
             nc.scalar.activation(out=warm[:], in_=one[:], func=ACT.Ln)
 
-            turned = psl.tile([P, 6, P], BF16, name="turned", tag="xl")
+            turned = psl.tile([P, 2, P], BF16, name="turned", tag="xl")
             for k in range(2):
                 nc.tensor.transpose(turned[:, k, :], rows[:, k:256:2], identb[:])
-            for k in range(4):
-                nc.tensor.transpose(turned[:, 2 + k, :], rows[:, k:512:4], identb[:])
             ips = [input_row(c) for c in range(2)]
             fps = {0: [hidden_row(0, c) for c in range(2)]}
-            pos = const.tile([P, 6, 14], F32)
+            turned_i = psl.tile([P, 4, P], BF16, name="turned_i", tag="xl")
+            for k in range(4):
+                nc.tensor.transpose(turned_i[:, k, :], rows[:, k:512:4], identb[:])
+            pos = const.tile([P, 2, 14], F32)
             nc.vector.tensor_copy(out=pos[:], in_=turned[:, :, 0:14])
             sop = const.tile([P, 2, 4], F32)
             nc.vector.tensor_scalar_mul(out=sop[:], in0=pos[:, 0:2, 10:14], scalar1=-RW)
@@ -181,12 +182,13 @@ def tile_physicalneuralnetwork_kernel(
 
             def input_biases():
                 nc.vector.tensor_scalar_mul(out=beta[:], in0=one[:], scalar1=KAP * BETA - 1.0)
-                posi = pos[:, 2:6, 0:2].rearrange("p (e c) u -> p c e u", c=2)
+                nc.vector.tensor_copy(out=posi[:], in_=turned_i[:, :, 0:2].rearrange("p (e c) u -> p c e u", c=2))
                 nc.vector.tensor_tensor(out=bi[:], in0=posi[:, 0], in1=posi[:, 1], op=ALU.add)
                 nc.vector.tensor_scalar(
                     out=bi[:], in0=bi[:], scalar1=-KAP * RW, scalar2=KAP * BETA - 1.0, op0=ALU.mult, op1=ALU.add
                 )
 
+            posi = const.tile([P, 2, 2, 2], F32)
             beta = const.tile([P, 1], F32)
             bi = const.tile([P, 2, 2], F32)
             psx[0] = psl
@@ -429,12 +431,13 @@ def tile_physicalneuralnetwork_kernel(
         quant_h(0, 0)
         quant_h(0, 1)
         quant_x(2)
-        l1_mm(1, range(0, 8))
+        l1_mm(1, range(0, 6))
+        for pair in (6, 7):
+            transposes(pair)
+        l1_mm(1, range(6, 8))
         regroup(1, 0)
         l2_mm(0, 0)
         l2_mm(0, 1)
-        for pair in (6, 7):
-            transposes(pair)
         regroup(1, 1, True)
         l1_mm(2, range(0, 4))
         for pair in (6, 7):

import itertools
from contextlib import ExitStack

import concourse.mybir as mybir
from concourse.masks import make_identity

F32 = mybir.dt.float32
BF16 = mybir.dt.bfloat16
U32 = mybir.dt.uint32
U8 = mybir.dt.uint8
FP8X4 = mybir.dt.float8_e4m3fn_x4
ACT = mybir.ActivationFunctionType
ALU = mybir.AluOpType

P = 128
B, I, H, O = 2048, 512, 1024, 512
FLOPS = 2 * B * I * H + 2 * B * H * O
WA = (5.0 - 0.09) / 6.0
BETA = (0.09 + (5.0 - 0.09) / 2.0) / WA
RW = 1.68e-8 / 35e-6 / WA
CH = 256
KAP = 16.0


def tile_physicalneuralnetwork_kernel(
    tc, x, W1, b1, W2, b2, input_positions, hidden_positions, output_positions, out
):
    nc = tc.nc
    with ExitStack() as ctx:
        const = ctx.enter_context(tc.tile_pool(name="const", bufs=1))
        w8 = ctx.enter_context(tc.tile_pool(name="w8", bufs=2))
        ctx.enter_context(tc.manual_schedule())
        ctx.enter_context(nc.allow_non_contiguous_dma(reason="small per-partition vectors"))

        rows = const.tile([P, 512], BF16)
        nc.vector.memset(rows[:].bitcast(U32), 0)
        one = const.tile([P, 1], F32)
        nc.vector.memset(one[:], 1.0)
        nc.sync.dma_start(out=rows[0:2, :], in_=input_positions.rearrange("(u r) c -> u (r c)", u=2))
        nc.sync.dma_start(out=rows[2:10, 0:256], in_=hidden_positions.rearrange("(a p) c -> a (p c)", p=P))
        nc.sync.dma_start(out=rows[10:14, 0:256], in_=output_positions.rearrange("(a p) c -> a (p c)", p=P))
        w1sb = const.tile([P, 4, H], BF16)
        for u in range(2):
            nc.sync.dma_start(
                out=w1sb[:, 2 * u : 2 * u + 2, :].rearrange("p e h -> p (e h)"),
                in_=W1[256 * u : 256 * u + 256, :].rearrange("(p e) h -> p (e h)", e=2),
            )
        biases = const.tile([P, 512], BF16)
        nc.gpsimd.memset(biases[:].bitcast(U32), 0)
        nc.sync.dma_start(out=biases[0:8, 0:128], in_=b1.rearrange("(a p) -> a p", p=P))
        nc.sync.dma_start(out=biases[8:9, :], in_=b2.rearrange("(a o) -> a o", a=1))
        w2sb = const.tile([P, 8, O], BF16)
        nc.sync.dma_start(out=w2sb[:], in_=W2.rearrange("(a p) o -> p a o", p=P))
        xsb = const.tile([P, 16, I], BF16)
        xv = x.rearrange("(m r) i -> m r i", r=16)
        for c in range(4):
            nc.sync.dma_start(out=xsb[:, 4 * c : 4 * c + 4, :], in_=xv[:, 4 * c : 4 * c + 4, :])

        identb = const.tile([P, P], BF16)
        make_identity(nc, identb[:])
        ident = const.tile([P, P], F32)
        make_identity(nc, ident[:])

        xg = const.tile([P, 16, P, 4], BF16, align_bytes=64)
        xc = const.tile([P, B], U32, align_bytes=64)
        xs = const.tile([P, B], U8, align_bytes=64)
        u1 = const.tile([P, 4, H], F32)
        u2 = const.tile([P, 8, O], F32)
        ll1 = const.tile([P, 4, H], F32)
        ll2 = const.tile([P, 8, O], F32)
        c1 = const.tile([P, 4 * CH], U32, align_bytes=64)
        s1 = const.tile([P, 4 * CH], U8, align_bytes=64)
        c2 = const.tile([P, 4 * CH], U32, align_bytes=64)
        s2 = const.tile([P, 4 * CH], U8, align_bytes=64)
        wc1 = w8.tile([P, 4, H], BF16, name="wc1", tag="w8", align_bytes=64)
        wc2 = w8.tile([P, 8, O], BF16, name="wc2", tag="w8", align_bytes=64)

        def clamp(layer, u):
            wc, wsb = (wc1, w1sb) if layer == 1 else (wc2, w2sb)
            n = wc.shape[1] // 2
            nc.vector.tensor_scalar(
                out=wc[:, n * u : n * u + n], in0=wsb[:, n * u : n * u + n], scalar1=-3.0, scalar2=3.0,
                op0=ALU.max, op1=ALU.min,
            )

        def numer(u, wc, wsb, q):
            cols = slice(1024 * q, 1024 * q + 1024)
            uv = u[:].rearrange("p j n -> p (j n)")[:, cols]
            cv = wc[:].rearrange("p j n -> p (j n)")[:, cols]
            wv = wsb[:].rearrange("p j n -> p (j n)")[:, cols]
            nc.vector.scalar_tensor_tensor(out=uv, in0=cv, scalar=BETA, in1=wv, op0=ALU.add, op1=ALU.mult)

        xts = {}

        def transposes(pair):
            xt = psx[0].tile([P, 2, 2, P], F32, name="xt", tag="xl")
            for rr in range(2):
                xw = xsb[:, 2 * pair + rr, :].bitcast(F32)
                for u in range(2):
                    nc.tensor.transpose(xt[:, rr, u, :], xw[:, P * u : P * u + P], ident[:])
            xts[pair] = xt

        def copy_x(pair, on_scalar):
            dst = xg[:].bitcast(F32)[:, 2 * pair : 2 * pair + 2]
            src = xts[pair][:].rearrange("p r u m -> p r m u")
            if on_scalar:
                nc.scalar.copy(out=dst, in_=src)
            else:
                nc.vector.tensor_copy(out=dst, in_=src)

        def quant_x(c):
            nc.vector.quantize_mx(
                out=xc[:, 512 * c : 512 * c + 512].bitcast(FP8X4),
                scales=xs[:, 512 * c : 512 * c + 512],
                in_=xg[:, 4 * c : 4 * c + 4].rearrange("p r m t -> p (r m t)"),
            )

        def recip(lv):
            nc.scalar.activation(out=lv, in_=lv, func=ACT.Sigmoid, scale=-1.0)

        def eff(ev, uv, lv):
            nc.vector.tensor_tensor(
                out=ev.rearrange("p (c i) t -> p c t i", i=4),
                in0=uv.rearrange("p t (c i) -> p c t i", i=4),
                in1=lv.rearrange("p t (c i) -> p c t i", i=4), op=ALU.mult,
            )

        def quant_w(e, cw, sw, k):
            nc.vector.quantize_mx(
                out=cw[:, CH * k : CH * k + CH].bitcast(FP8X4),
                scales=sw[:, CH * k : CH * k + CH],
                in_=e[:, k].rearrange("p h t -> p (h t)"),
            )

        psx = {}
        with tc.psum_pool(name="psp", bufs=1) as psp, tc.psum_pool(name="psl", bufs=6) as psl, tc.tile_pool(
            name="pl", bufs=8
        ) as pl:
            def spread(out, row, src):
                nc.tensor.matmul(
                    out=out, lhsT=identb[:, row : row + 1].to_broadcast([P, P]), rhs=src, start=True, stop=True
                )

            def hidden_row(hh, c):
                t = psp.tile([P, 4, P], F32, name="fp", tag="f" + "xy"[c])
                for g in range(4):
                    spread(t[:, g], 2 + 4 * hh + g, rows[:, c:256:2])
                return t

            def input_row(c):
                t = psl.tile([P, 4, P], F32, name="ip", tag="xl")
                for k in range(4):
                    spread(t[:, k], k // 2, rows[:, 2 * (k % 2) + c : 512 : 4])
                return t

            warm = const.tile([P, 1], F32)
            nc.scalar.activation(out=warm[:], in_=one[:], func=ACT.Ln)

            turned = psl.tile([P, 2, P], BF16, name="turned", tag="xl")
            for k in range(2):
                nc.tensor.transpose(turned[:, k, :], rows[:, k:256:2], identb[:])
            ips = [input_row(c) for c in range(2)]
            fps = {0: [hidden_row(0, c) for c in range(2)]}
            turned_i = psl.tile([P, 4, P], BF16, name="turned_i", tag="xl")
            for k in range(4):
                nc.tensor.transpose(turned_i[:, k, :], rows[:, k:512:4], identb[:])
            pos = const.tile([P, 2, 14], F32)
            nc.vector.tensor_copy(out=pos[:], in_=turned[:, :, 0:14])
            sop = const.tile([P, 2, 4], F32)
            nc.vector.tensor_scalar_mul(out=sop[:], in0=pos[:, 0:2, 10:14], scalar1=-RW)
            hp2 = const.tile([P, 2, 8], F32)
            nc.vector.tensor_scalar_mul(out=hp2[:], in0=pos[:, 0:2, 2:10], scalar1=2.0 * RW)
            hp1 = const.tile([P, 2, 8], F32)
            nc.vector.tensor_scalar_mul(out=hp1[:], in0=pos[:, 0:2, 2:10], scalar1=RW)
            ixy = []
            for c in range(2):
                it = const.tile([P, 512], F32, name="i" + "xy"[c])
                nc.scalar.activation(
                    out=it[:], in_=ips[c][:].rearrange("p t n -> p (t n)"), func=ACT.Copy, scale=2.0 * RW
                )
                ixy.append(it)

            def input_biases():
                nc.vector.tensor_scalar_mul(out=beta[:], in0=one[:], scalar1=KAP * BETA - 1.0)
                nc.vector.tensor_copy(out=posi[:], in_=turned_i[:, :, 0:2].rearrange("p (e c) u -> p c e u", c=2))
                nc.vector.tensor_tensor(out=bi[:], in0=posi[:, 0], in1=posi[:, 1], op=ALU.add)
                nc.vector.tensor_scalar(
                    out=bi[:], in0=bi[:], scalar1=-KAP * RW, scalar2=KAP * BETA - 1.0, op0=ALU.mult, op1=ALU.add
                )

            posi = const.tile([P, 2, 2, 2], F32)
            beta = const.tile([P, 1], F32)
            bi = const.tile([P, 2, 2], F32)
            psx[0] = psl
            parts = {}

            def part_v(hh, g, c):
                a = 4 * hh + g
                t = pl.tile([P, 512], F32, name="pv", bufs=16)
                nc.vector.tensor_scalar(
                    out=t[:], in0=ixy[c][:], scalar1=hp2[:, c, a : a + 1], scalar2=hp1[:, c, a : a + 1],
                    op0=ALU.max, op1=ALU.subtract,
                )
                parts[1, hh, g, c] = t

            def part_s(hh, g, c):
                t = pl.tile([P, 512], F32, name="ps", bufs=16)
                nc.scalar.activation(
                    out=t[:], in_=fps[hh][c][:].rearrange("p g n -> p (g n)"), func=ACT.Abs, bias=sop[:, c, g : g + 1], scale=RW
                )
                parts[2, hh, g, c] = t

            sums = {}

            def totals(layer, hh, blocks, clip_first):
                for t in blocks:
                    sums[layer, hh, t] = psl.tile([P, 4, P], F32, name="xl")

                def turn(t, g, c):
                    first, last = g == 0 and c == 0, g == 3 and c == 1
                    nc.tensor.matmul(
                        out=sums[layer, hh, t][:, g, :], lhsT=parts[layer, hh, g, c][:, P * t : P * t + P],
                        rhs=ident[:], is_transpose=True, start=first and not clip_first, stop=last and clip_first,
                    )

                def add_clip(t):
                    wcv = wc1[:, t, 512 * hh : 512 * hh + 512] if layer == 1 else wc2[:, 4 * hh + t, :]
                    nc.tensor.matmul(
                        out=sums[layer, hh, t][:], lhsT=identb[:], rhs=wcv, start=clip_first, stop=not clip_first
                    )

                if clip_first:
                    for t in blocks:
                        add_clip(t)
                    for t, c, g in itertools.product(blocks, range(2), range(4)):
                        turn(t, g, c)
                else:
                    for c, g, t in itertools.product(range(2), range(4), blocks):
                        turn(t, g, c)
                    for t in blocks:
                        add_clip(t)

            def log(layer, hh, t):
                if layer == 1:
                    lv, bias = ll1[:, t, 512 * hh : 512 * hh + 512], bi[:, t % 2, t // 2 : t // 2 + 1]
                else:
                    lv, bias = ll2[:, 4 * hh + t, :], beta[:]
                nc.scalar.activation(out=lv, in_=sums[layer, hh, t][:], func=ACT.Ln, bias=bias, scale=KAP)

            b2b = const.tile([P, O], F32)
            for c, g in itertools.product(range(2), range(4)):
                part_s(0, g, c)
            for c, g in itertools.product(range(2), range(4)):
                part_v(0, g, c)
            input_biases()
            clamp(1, 0)
            clamp(1, 1)
            totals(1, 0, range(4), False)
            for t in range(4):
                log(1, 0, t)
            fps[1] = [hidden_row(1, c) for c in range(2)]
            clamp(2, 0)
            clamp(2, 1)
            totals(2, 0, range(4), True)
            transposes(0)
            transposes(1)
            for c, g in itertools.product(range(2), range(4)):
                part_v(1, g, c)
            for t in range(4):
                log(2, 0, t)
            for c, g in itertools.product(range(2), range(4)):
                part_s(1, g, c)
            numer(u1, wc1, w1sb, 0)
            numer(u1, wc1, w1sb, 1)
            copy_x(0, False)
            copy_x(1, False)
            numer(u1, wc1, w1sb, 2)
            numer(u1, wc1, w1sb, 3)
            quant_x(0)
            totals(1, 1, range(4), False)
            for t in range(4):
                log(1, 1, t)
            for q in range(4):
                numer(u2, wc2, w2sb, q)
            totals(2, 1, range(0, 2), True)
            totals(2, 1, range(2, 4), True)
            for t in range(4):
                log(2, 1, t)
            for pair in (2, 3):
                transposes(pair)
                copy_x(pair, False)
            b1t = psl.tile([P, P], BF16, name="b1t", tag="xl")
            nc.tensor.transpose(b1t[:], biases[:, 0:P], identb[:])
            b2p = psl.tile([P, O], F32, name="b2p", tag="xl")
            spread(b2p[:], 8, biases[:])
            quant_x(1)
            b1f = const.tile([P, 8], F32)
            nc.vector.tensor_copy(out=b1f[:], in_=b1t[:, 0:8])
            nc.vector.tensor_copy(out=b2b[:], in_=b2p[:])

        psa = ctx.enter_context(tc.psum_pool(name="psa", bufs=4))
        psb = ctx.enter_context(tc.psum_pool(name="psb", bufs=4))
        psx[0] = psb
        hp = ctx.enter_context(tc.tile_pool(name="hp", bufs=2))
        hq = ctx.enter_context(tc.tile_pool(name="hq", bufs=3))
        op = ctx.enter_context(tc.tile_pool(name="op", bufs=10))

        e1 = w8.tile([P, 4, CH, 4], BF16, name="e1", tag="w8", align_bytes=64)
        e2 = w8.tile([P, 4, CH, 4], BF16, name="e2", tag="w8", align_bytes=64)

        def view2(t, k):
            g, oh = k // 2, k % 2
            return t[:, 4 * g : 4 * g + 4, CH * oh : CH * oh + CH]

        def eff1(lo, n):
            cols = slice(lo, lo + n)
            eff(e1[:].rearrange("p k n t -> p (k n) t")[:, cols], u1[:, :, cols], ll1[:, :, cols])

        def eff2(k):
            eff(e2[:, k], view2(u2, k), view2(ll2, k))

        ov = out.rearrange("(m r) o -> m r o", r=16)
        hid = {}

        def l1_mm(c, mts):
            if c not in hid:
                hc = hp.tile([P, 8, 512], BF16, name="hc")
                gc = hp.tile([P, 2, 512, 4], BF16, name="gc", align_bytes=64)
                cc = hq.tile([P, 2, 512], U32, name="cc", align_bytes=64)
                sc = hq.tile([P, 2, 512], U8, name="sc", align_bytes=64)
                hid[c] = (hc, gc, cc, sc)
            hc = hid[c][0]
            for mt in mts:
                ps = psa.tile([P, 512], F32, name="ps")
                nc.tensor.matmul_mx(
                    out=ps[:],
                    lhsT=c1[:, P * mt : P * mt + P].bitcast(FP8X4),
                    lhsT_scale=s1[:, P * mt : P * mt + P],
                    rhs=xc[:, 512 * c : 512 * c + 512].bitcast(FP8X4),
                    rhs_scale=xs[:, 512 * c : 512 * c + 512],
                    start=True, stop=True,
                )
                nc.scalar.activation(
                    out=hc[:, mt, :], in_=ps[:], func=ACT.Sigmoid, bias=b1f[:, mt : mt + 1], scale=KAP
                )

        def regroup(c, g, on_gpsimd=False):
            hc, gc = hid[c][0], hid[c][1]
            if on_gpsimd:
                nc.gpsimd.tensor_scalar(
                    out=gc[:, g], in0=hc[:, 4 * g : 4 * g + 4, :].rearrange("p t n -> p n t"), scalar1=1.0, scalar2=0.0,
                    op0=ALU.mult, op1=ALU.add,
                )
            else:
                nc.vector.tensor_copy(
                    out=gc[:, g].rearrange("p (c i) t -> p c t i", i=4),
                    in_=hc[:, 4 * g : 4 * g + 4, :].rearrange("p t (c i) -> p c t i", i=4),
                )

        def quant_h(c, g):
            gc, cc, sc = hid[c][1], hid[c][2], hid[c][3]
            nc.vector.quantize_mx(
                out=cc[:, g].bitcast(FP8X4), scales=sc[:, g], in_=gc[:, g].rearrange("p b t -> p (b t)")
            )

        outs = {}

        sums2 = {}

        def l2_pass(c, rr, g):
            cc, sc = hid[c][2], hid[c][3]
            if g == 0:
                sums2[c, rr] = psa.tile([P, 512], F32, name="ps") if c == 3 else psb.tile(
                    [P, 512], F32, name="ps2", tag="xl"
                )
            nc.tensor.matmul_mx(
                out=sums2[c, rr][:],
                lhsT=cc[:, g, P * rr : P * rr + P].bitcast(FP8X4),
                lhsT_scale=sc[:, g, P * rr : P * rr + P],
                rhs=c2[:, 512 * g : 512 * g + 512].bitcast(FP8X4),
                rhs_scale=s2[:, 512 * g : 512 * g + 512],
                start=(g == 0), stop=(g == 1),
            )

        def out_columns(c, rr):
            return (slice(0, 256), slice(256, 512)) if (c, rr) == (3, 3) else (slice(0, 512),)

        def l2_add(c, rr):
            ot = op.tile([P, 512], F32, name="ot")
            outs[(c, rr)] = ot
            for cols in out_columns(c, rr):
                nc.vector.scalar_tensor_tensor(
                    out=ot[:, cols], in0=sums2[c, rr][:, cols], scalar=KAP, in1=b2b[:, cols], op0=ALU.mult, op1=ALU.add
                )

        def l2_mm(c, rr):
            l2_pass(c, rr, 0)
            l2_pass(c, rr, 1)
            l2_add(c, rr)

        def l2_out(c, rr):
            ot = outs[(c, rr)]
            for cols in out_columns(c, rr):
                nc.scalar.activation(out=ot[:, cols], in_=ot[:, cols], func=ACT.Sigmoid)
                nc.sync.dma_start(out=ov[:, 4 * c + rr, cols], in_=ot[:, cols])

        pieces = [(0, CH // 2), (CH // 2, CH // 2)] + [(CH * k, CH) for k in range(1, 4)]
        for lo, n in pieces:
            recip(ll1[:, :, lo : lo + n])
        for k in range(4):
            recip(view2(ll2, k))
        eff1(*pieces[0])
        eff1(*pieces[1])
        quant_w(e1, c1, s1, 0)
        eff1(*pieces[2])
        for k in range(1, 3):
            eff1(*pieces[k + 2])
            quant_w(e1, c1, s1, k)
        eff2(0)
        quant_w(e1, c1, s1, 3)
        for k in range(1, 4):
            eff2(k)
            quant_w(e2, c2, s2, k - 1)
        l1_mm(0, range(0, 8))
        for pair in (4, 5):
            transposes(pair)
            copy_x(pair, True)
        regroup(0, 0)
        quant_w(e2, c2, s2, 3)
        regroup(0, 1)
        quant_h(0, 0)
        quant_h(0, 1)
        quant_x(2)
        l1_mm(1, range(0, 6))
        for pair in (6, 7):
            transposes(pair)
        l1_mm(1, range(6, 8))
        regroup(1, 0)
        l2_mm(0, 0)
        l2_mm(0, 1)
        regroup(1, 1, True)
        l1_mm(2, range(0, 4))
        for pair in (6, 7):
            copy_x(pair, False)
        l2_mm(0, 2)
        l2_mm(0, 3)
        quant_h(1, 0)
        quant_h(1, 1)
        quant_x(3)
        l1_mm(2, range(4, 8))
        for rr in range(4):
            l2_out(0, rr)
        regroup(2, 0)
        regroup(2, 1, True)
        l2_mm(1, 0)
        l2_mm(1, 1)
        l1_mm(3, range(0, 4))
        l2_mm(1, 2)
        l2_mm(1, 3)
        quant_h(2, 0)
        quant_h(2, 1)
        l1_mm(3, range(4, 8))
        for rr in range(4):
            l2_out(1, rr)
        regroup(3, 0)
        l2_mm(2, 0)
        quant_h(3, 0)
        l2_mm(2, 1)
        regroup(3, 1)
        for rr in range(4):
            l2_pass(3, rr, 0)
        l2_mm(2, 2)
        quant_h(3, 1)
        l2_mm(2, 3)
        for rr in range(4):
            l2_out(2, rr)
        for rr in range(4):
            l2_pass(3, rr, 1)
            l2_add(3, rr)
            l2_out(3, rr)
